import numpy as np
import ml_dtypes


def mxq(x, axis, fmt="e4m3"):
    dtype, down = {"e4m3": (ml_dtypes.float8_e4m3fn, 7), "e5m2": (ml_dtypes.float8_e5m2, 14)}[fmt]
    v = np.moveaxis(np.asarray(x, np.float32).astype(ml_dtypes.bfloat16).astype(np.float64), axis, -1)
    blocks = v.reshape(v.shape[:-1] + (-1, 32))
    amax = np.abs(blocks).max(-1, keepdims=True)
    byte = np.maximum(np.where(amax > 0, np.frexp(amax)[1] - 1 + 127, 0) - down, 1)
    scale = np.exp2(byte - 127.0)
    codes = (blocks / scale).astype(np.float32).astype(dtype).astype(np.float64)
    return np.moveaxis((codes * scale).reshape(v.shape), -1, axis)


WIDE = False


def mx_kscale(k):
    if not WIDE:
        return np.ones(k)
    levels = np.array([10, -10, 5, -5, 0])
    a = np.random.permutation(np.resize(levels, k // 512 * 4)).reshape(k // 512, 4)
    idx = np.arange(k)
    return np.exp2(a[idx // 512, idx % 128 // 32])


BF16 = ml_dtypes.bfloat16


def bf(x):
    return np.asarray(x, np.float32).astype(BF16)


def f64(x):
    return np.asarray(x).astype(np.float64)


B, A, S, R, H = 512, 32, 512, 1024, 1024


def sigmoid(v):
    return 1.0 / (1.0 + np.exp(-v))


def elu(v):
    return np.where(v > 0.0, v, np.exp(np.minimum(v, 0.0)) - 1.0)


def setup_inputs():
    s = mx_kscale(H)
    return {"h": bf(elu(np.random.standard_normal((B, H))) * s),
            "prev_rnn_hidden": bf(np.random.standard_normal((B, R))),
            "W_ih": bf(np.random.standard_normal((3 * R, H)) / np.sqrt(H) / s[None, :]),
            "W_hh": bf(np.random.standard_normal((3 * R, R)) / np.sqrt(R)),
            "b_ih": bf(np.random.standard_normal(3 * R) * 0.3),
            "b_n": bf(np.random.standard_normal(R) * 0.3)}


def reference(h, prev_rnn_hidden, W_ih, W_hh, b_ih, b_n):
    hp = f64(prev_rnn_hidden)
    igates = (mxq(f64(h), 1, "e4m3") @ mxq(f64(W_ih), 1, "e4m3").T) + f64(b_ih)
    hgates = mxq(hp, 1, "e4m3") @ mxq(f64(W_hh), 1, "e4m3").T
    ig_r, ig_z, ig_n = np.split(igates, 3, axis=-1)
    hg_r, hg_z, hg_n = np.split(hgates, 3, axis=-1)
    reset = sigmoid(ig_r + hg_r)
    update = sigmoid(ig_z + hg_z)
    new = np.tanh(ig_n + reset * (hg_n + f64(b_n)))
    return new + update * (hp - new)

@@ -1,0 +1,208 @@
+from contextlib import ExitStack
+
+import concourse.mybir as mybir
+from concourse.masks import make_identity
+
+F32 = mybir.dt.float32
+BF16 = mybir.dt.bfloat16
+U32 = mybir.dt.uint32
+U8 = mybir.dt.uint8
+FP8X4 = mybir.dt.float8_e4m3fn_x4
+ACT = mybir.ActivationFunctionType
+ALU = mybir.AluOpType
+
+P = 128
+BATCH = 512
+K = 1024
+R = 1024
+K_PASS = 4 * P
+PASSES = K // K_PASS
+WORDS = K // 2
+CHUNKS = WORDS // P
+ROW_TILES = BATCH // P
+COL_TILES = R // P
+GATE_R, GATE_Z, GATE_N = 0, 1, 2
+BLOCKS = [("ih", GATE_R), ("hh", GATE_R), ("hh", GATE_N), ("ih", GATE_N), ("ih", GATE_Z), ("hh", GATE_Z)]
+HALF = len(BLOCKS) // 2
+BLOCK_WORDS = PASSES * P
+FLOPS = 2 * 2 * BATCH * 3 * R * K
+
+
+def tile_prior_pa_kernel(tc, h, prev_rnn_hidden, W_ih, W_hh, b_ih, b_n, out):
+    nc = tc.nc
+    with ExitStack() as ctx:
+        ctx.enter_context(tc.manual_schedule())
+        const = ctx.enter_context(tc.tile_pool(name="const", bufs=1))
+        acts = ctx.enter_context(tc.tile_pool(name="acts", bufs=1))
+        rows_pool = ctx.enter_context(tc.tile_pool(name="rows", bufs=COL_TILES))
+        stage = ctx.enter_context(tc.tile_pool(name="stage", bufs=4))
+        quantised = ctx.enter_context(tc.tile_pool(name="quantised", bufs=2))
+        gates = ctx.enter_context(tc.tile_pool(name="gates", bufs=2))
+        psum = ctx.enter_context(tc.psum_pool(name="psum", bufs=8))
+
+        bias_rows = const.tile([P, P], BF16)
+        nc.vector.memset(bias_rows[:], 0.0)
+        zero = const.tile([P, 1], F32)
+        nc.vector.memset(zero[:], 0.0)
+        nc.scalar.dma_start(out=bias_rows[0:24, :], in_=b_ih.rearrange("(r c) -> r c", c=P))
+        nc.scalar.dma_start(out=bias_rows[24:32, :], in_=b_n.rearrange("(r c) -> r c", c=P))
+        warm = const.tile([P, 1], F32)
+        nc.scalar.activation(out=warm[:], in_=zero[:], func=ACT.Sigmoid)
+        ident = const.tile([P, P], F32)
+        make_identity(nc, ident[:])
+
+        inputs = {"ih": h, "hh": prev_rnn_hidden}
+        weights = {"ih": W_ih, "hh": W_hh}
+        act_rows = {}
+        for src in ("ih", "hh"):
+            rows = acts.tile([P, ROW_TILES * K], BF16, name="act_rows_" + src)
+            act_rows[src] = rows
+            for m in range(ROW_TILES):
+                nc.sync.dma_start(out=rows[:, m * K : (m + 1) * K], in_=inputs[src][m * P : (m + 1) * P, :])
+        w_rows = []
+        for t in range(COL_TILES):
+            rows = rows_pool.tile([P, len(BLOCKS) * K], BF16, tag="w_rows", name="w_rows")
+            w_rows.append(rows)
+            for pos, (src, gate) in enumerate(BLOCKS):
+                first = gate * R + t * P
+                nc.sync.dma_start(out=rows[:, pos * K : (pos + 1) * K], in_=weights[src][first : first + P, :])
+
+        def flip(words):
+            flipped = psum.tile([P, WORDS], F32, tag="bank")
+            for c in range(CHUNKS):
+                cols = slice(c * P, (c + 1) * P)
+                nc.tensor.transpose(flipped[:, cols], words[:, cols], ident[:])
+            return flipped[:].rearrange("p (g u r) -> p g r u", g=PASSES, u=2)
+
+        act_codes = {}
+        act_scales = {}
+        for src in ("ih", "hh"):
+            grouped = acts.tile([P, PASSES * BATCH * 4], BF16, align_bytes=64, name="act_grouped_" + src)
+            by_tile = grouped[:].bitcast(F32).rearrange("p (g m r u) -> p g m r u", g=PASSES, m=ROW_TILES, u=2)
+            for m in range(ROW_TILES):
+                flipped = flip(act_rows[src][:].bitcast(F32)[:, m * WORDS : (m + 1) * WORDS])
+                if m % 2 == 0:
+                    nc.scalar.copy(out=by_tile[:, :, m], in_=flipped)
+                else:
+                    nc.vector.tensor_copy(out=by_tile[:, :, m], in_=flipped)
+            codes = acts.tile([P, PASSES * BATCH], U32, align_bytes=64, name="act_codes_" + src)
+            scales = acts.tile([P, PASSES * BATCH], U8, align_bytes=64, name="act_scales_" + src)
+            for g in range(PASSES):
+                cols = slice(g * BATCH, (g + 1) * BATCH)
+                nc.vector.quantize_mx(
+                    out=codes[:, cols].bitcast(FP8X4),
+                    scales=scales[:, cols],
+                    in_=grouped[:, 4 * g * BATCH : 4 * (g + 1) * BATCH],
+                )
+            act_codes[src] = codes
+            act_scales[src] = scales
+
+        bias_f32 = const.tile([P, P], F32)
+        nc.vector.tensor_copy(out=bias_f32[:], in_=bias_rows[:])
+        bias_bank = psum.tile([P, WORDS], F32, tag="bank")
+        nc.tensor.transpose(bias_bank[:, 0:P], bias_f32[:], ident[:])
+        bias = const.tile([P, 32], F32)
+        nc.vector.tensor_copy(out=bias[:], in_=bias_bank[:, 0:32])
+
+        w_codes = {}
+        w_scales = {}
+
+        def quantise_weight_blocks(t, positions):
+            if t not in w_codes:
+                codes = quantised.tile([P, len(BLOCKS) * BLOCK_WORDS], U32, align_bytes=64, tag="w_codes")
+                scales = quantised.tile([P, len(BLOCKS) * BLOCK_WORDS], U8, align_bytes=64, tag="w_scales")
+                w_codes[t] = codes
+                w_scales[t] = scales
+            for pos in positions:
+                flipped = flip(w_rows[t][:].bitcast(F32)[:, pos * WORDS : (pos + 1) * WORDS])
+                grouped = stage.tile([P, K], BF16, align_bytes=64)
+                nc.scalar.copy(
+                    out=grouped[:].bitcast(F32).rearrange("p (g r u) -> p g r u", g=PASSES, u=2), in_=flipped
+                )
+                cols = slice(pos * BLOCK_WORDS, (pos + 1) * BLOCK_WORDS)
+                nc.vector.quantize_mx(
+                    out=w_codes[t][:, cols].bitcast(FP8X4), scales=w_scales[t][:, cols], in_=grouped[:]
+                )
+
+        def multiply(t, gate, sources):
+            acc = psum.tile([P, BATCH], F32, tag="bank")
+            passes = [(src, g) for src in sources for g in range(PASSES)]
+            for i, (src, g) in enumerate(passes):
+                first = BLOCKS.index((src, gate)) * BLOCK_WORDS + g * P
+                w_cols = slice(first, first + P)
+                a_cols = slice(g * BATCH, (g + 1) * BATCH)
+                nc.tensor.matmul_mx(
+                    out=acc[:],
+                    lhsT=w_codes[t][:, w_cols].bitcast(FP8X4),
+                    lhsT_scale=w_scales[t][:, w_cols],
+                    rhs=act_codes[src][:, a_cols].bitcast(FP8X4),
+                    rhs_scale=act_scales[src][:, a_cols],
+                    start=(i == 0),
+                    stop=(i == len(passes) - 1),
+                )
+            return acc
+
+        def flip_back(values):
+            back = psum.tile([P, BATCH], F32, tag="bank")
+            for m in range(ROW_TILES):
+                cols = slice(m * P, (m + 1) * P)
+                nc.tensor.transpose(back[:, cols], values[:, cols], ident[:])
+            return back[:].rearrange("p (m j) -> p m j", m=ROW_TILES)
+
+        hp_by_tile = act_rows["hh"][:].rearrange("p (m k) -> p m k", m=ROW_TILES)
+        out_by_tile = out.rearrange("(m p) j -> p m j", p=P)
+
+        def blend(t, new_back, update_back):
+            cols = slice(t * P, (t + 1) * P)
+            diff = gates.tile([P, ROW_TILES, P], F32)
+            nc.vector.tensor_tensor(out=diff[:], in0=hp_by_tile[:, :, cols], in1=new_back, op=ALU.subtract)
+            step = gates.tile([P, ROW_TILES, P], F32)
+            nc.vector.scalar_tensor_tensor(
+                out=step[:], in0=update_back, scalar=-1.0, in1=diff[:], op0=ALU.add, op1=ALU.mult
+            )
+            result = gates.tile([P, ROW_TILES, P], F32)
+            nc.vector.tensor_tensor(out=result[:], in0=hp_by_tile[:, :, cols], in1=step[:], op=ALU.add)
+            nc.sync.dma_start(out=out_by_tile[:, :, cols], in_=result[:])
+
+        def bias_column(index):
+            return bias[:, index : index + 1]
+
+        quantise_weight_blocks(0, range(len(BLOCKS)))
+        new = {}
+        update = {}
+        for t in range(COL_TILES):
+            acc_r = multiply(t, GATE_R, ("ih", "hh"))
+            reset = gates.tile([P, BATCH], F32)
+            nc.scalar.activation(out=reset[:], in_=acc_r[:], func=ACT.Sigmoid, bias=bias_column(8 * GATE_R + t))
+            acc_hn = multiply(t, GATE_N, ("hh",))
+            gated = gates.tile([P, BATCH], F32)
+            nc.vector.scalar_tensor_tensor(
+                out=gated[:], in0=acc_hn[:], scalar=bias_column(24 + t), in1=reset[:], op0=ALU.add, op1=ALU.mult
+            )
+
+            if t + 1 < COL_TILES:
+                quantise_weight_blocks(t + 1, range(0, HALF))
+            if t > 0:
+                new_back = flip_back(new[t - 1])
+                update_back = flip_back(update[t - 1])
+
+            acc_in = multiply(t, GATE_N, ("ih",))
+            pre = gates.tile([P, BATCH], F32)
+            nc.vector.tensor_tensor(out=pre[:], in0=acc_in[:], in1=gated[:], op=ALU.add)
+            new_t = gates.tile([P, BATCH], F32)
+            nc.scalar.activation(out=new_t[:], in_=pre[:], func=ACT.Tanh, bias=bias_column(8 * GATE_N + t))
+            new[t] = new_t
+            acc_z = multiply(t, GATE_Z, ("ih", "hh"))
+            update_t = gates.tile([P, BATCH], F32)
+            nc.scalar.activation(out=update_t[:], in_=acc_z[:], func=ACT.Sigmoid, bias=bias_column(8 * GATE_Z + t))
+            update[t] = update_t
+
+            if t > 0:
+                blend(t - 1, new_back, update_back)
+            if t + 1 < COL_TILES:
+                quantise_weight_blocks(t + 1, range(HALF, len(BLOCKS)))
+
+        last = COL_TILES - 1
+        new_back = flip_back(new[last])
+        update_back = flip_back(update[last])
+        blend(last, new_back, update_back)

@@ -21,6 +21,7 @@ WORDS = K // 2
 CHUNKS = WORDS // P
 ROW_TILES = BATCH // P
 COL_TILES = R // P
+PAIRS = COL_TILES // 2
 GATE_R, GATE_Z, GATE_N = 0, 1, 2
 BLOCKS = [("ih", GATE_R), ("hh", GATE_R), ("hh", GATE_N), ("ih", GATE_N), ("ih", GATE_Z), ("hh", GATE_Z)]
 HALF = len(BLOCKS) // 2
@@ -40,12 +41,12 @@ def tile_prior_pa_kernel(tc, h, prev_rnn_hidden, W_ih, W_hh, b_ih, b_n, out):
         gates = ctx.enter_context(tc.tile_pool(name="gates", bufs=2))
         psum = ctx.enter_context(tc.psum_pool(name="psum", bufs=8))
 
-        bias_rows = const.tile([P, P], BF16)
+        bias_rows = const.tile([P, 2 * P], BF16)
         nc.vector.memset(bias_rows[:], 0.0)
         zero = const.tile([P, 1], F32)
         nc.vector.memset(zero[:], 0.0)
-        nc.scalar.dma_start(out=bias_rows[0:24, :], in_=b_ih.rearrange("(r c) -> r c", c=P))
-        nc.scalar.dma_start(out=bias_rows[24:32, :], in_=b_n.rearrange("(r c) -> r c", c=P))
+        nc.scalar.dma_start(out=bias_rows[0:12, :], in_=b_ih.rearrange("(r c) -> r c", c=2 * P))
+        nc.scalar.dma_start(out=bias_rows[12:16, :], in_=b_n.rearrange("(r c) -> r c", c=2 * P))
         warm = const.tile([P, 1], F32)
         nc.scalar.activation(out=warm[:], in_=zero[:], func=ACT.Sigmoid)
         ident = const.tile([P, P], F32)
@@ -63,28 +64,45 @@ def tile_prior_pa_kernel(tc, h, prev_rnn_hidden, W_ih, W_hh, b_ih, b_n, out):
         for t in range(COL_TILES):
             rows = rows_pool.tile([P, len(BLOCKS) * K], BF16, tag="w_rows", name="w_rows")
             w_rows.append(rows)
+            c, e = divmod(t, 2)
             for pos, (src, gate) in enumerate(BLOCKS):
-                first = gate * R + t * P
-                nc.sync.dma_start(out=rows[:, pos * K : (pos + 1) * K], in_=weights[src][first : first + P, :])
+                first = gate * R + c * 2 * P
+                both = weights[src][first : first + 2 * P, :].rearrange("(p e) k -> p e k", e=2)
+                nc.sync.dma_start(out=rows[:, pos * K : (pos + 1) * K], in_=both[:, e, :])
 
         def flip(words):
             flipped = psum.tile([P, WORDS], F32, tag="bank")
             for c in range(CHUNKS):
                 cols = slice(c * P, (c + 1) * P)
                 nc.tensor.transpose(flipped[:, cols], words[:, cols], ident[:])
-            return flipped[:].rearrange("p (g u r) -> p g r u", g=PASSES, u=2)
+            return flipped
 
         act_codes = {}
         act_scales = {}
+        act_grouped = {}
         for src in ("ih", "hh"):
             grouped = acts.tile([P, PASSES * BATCH * 4], BF16, align_bytes=64, name="act_grouped_" + src)
-            by_tile = grouped[:].bitcast(F32).rearrange("p (g m r u) -> p g m r u", g=PASSES, m=ROW_TILES, u=2)
+            act_grouped[src] = grouped
             for m in range(ROW_TILES):
                 flipped = flip(act_rows[src][:].bitcast(F32)[:, m * WORDS : (m + 1) * WORDS])
-                if m % 2 == 0:
-                    nc.scalar.copy(out=by_tile[:, :, m], in_=flipped)
+                copy = nc.scalar.copy if m % 2 == 0 else nc.vector.tensor_copy
+                if src == "ih":
+                    copy(
+                        out=grouped[:]
+                        .bitcast(F32)
+                        .rearrange("p (g m r u) -> p g m r u", g=PASSES, m=ROW_TILES, u=2)[:, :, m],
+                        in_=flipped[:].rearrange("p (g u r) -> p g r u", g=PASSES, u=2),
+                    )
                 else:
-                    nc.vector.tensor_copy(out=by_tile[:, :, m], in_=flipped)
+                    for g in range(PASSES):
+                        copy(
+                            out=grouped[:].rearrange(
+                                "p (g m r u e) -> p g m r u e", g=PASSES, m=ROW_TILES, u=2, e=2
+                            )[:, g, m],
+                            in_=flipped[:]
+                            .bitcast(BF16)
+                            .rearrange("p (g u r e) -> p g r u e", g=PASSES, u=2, e=2)[:, g],
+                        )
             codes = acts.tile([P, PASSES * BATCH], U32, align_bytes=64, name="act_codes_" + src)
             scales = acts.tile([P, PASSES * BATCH], U8, align_bytes=64, name="act_scales_" + src)
             for g in range(PASSES):
@@ -97,12 +115,15 @@ def tile_prior_pa_kernel(tc, h, prev_rnn_hidden, W_ih, W_hh, b_ih, b_n, out):
             act_codes[src] = codes
             act_scales[src] = scales
 
-        bias_f32 = const.tile([P, P], F32)
-        nc.vector.tensor_copy(out=bias_f32[:], in_=bias_rows[:])
+        bias_parted = const.tile([P, 2, P], F32)
+        nc.vector.tensor_copy(out=bias_parted[:], in_=bias_rows[:].rearrange("r (p e) -> r e p", e=2))
         bias_bank = psum.tile([P, WORDS], F32, tag="bank")
-        nc.tensor.transpose(bias_bank[:, 0:P], bias_f32[:], ident[:])
-        bias = const.tile([P, 32], F32)
-        nc.vector.tensor_copy(out=bias[:], in_=bias_bank[:, 0:32])
+        for e in range(2):
+            nc.tensor.transpose(bias_bank[:, e * P : (e + 1) * P], bias_parted[:, e, :], ident[:])
+        bias = const.tile([P, 2, 16], F32)
+        nc.vector.tensor_copy(
+            out=bias[:], in_=bias_bank[:, 0 : 2 * P].rearrange("p (e r) -> p e r", e=2)[:, :, 0:16]
+        )
 
         w_codes = {}
         w_scales = {}
@@ -117,7 +138,8 @@ def tile_prior_pa_kernel(tc, h, prev_rnn_hidden, W_ih, W_hh, b_ih, b_n, out):
                 flipped = flip(w_rows[t][:].bitcast(F32)[:, pos * WORDS : (pos + 1) * WORDS])
                 grouped = stage.tile([P, K], BF16, align_bytes=64)
                 nc.scalar.copy(
-                    out=grouped[:].bitcast(F32).rearrange("p (g r u) -> p g r u", g=PASSES, u=2), in_=flipped
+                    out=grouped[:].bitcast(F32).rearrange("p (g r u) -> p g r u", g=PASSES, u=2),
+                    in_=flipped[:].rearrange("p (g u r) -> p g r u", g=PASSES, u=2),
                 )
                 cols = slice(pos * BLOCK_WORDS, (pos + 1) * BLOCK_WORDS)
                 nc.vector.quantize_mx(
@@ -142,67 +164,84 @@ def tile_prior_pa_kernel(tc, h, prev_rnn_hidden, W_ih, W_hh, b_ih, b_n, out):
                 )
             return acc
 
-        def flip_back(values):
-            back = psum.tile([P, BATCH], F32, tag="bank")
-            for m in range(ROW_TILES):
-                cols = slice(m * P, (m + 1) * P)
-                nc.tensor.transpose(back[:, cols], values[:, cols], ident[:])
-            return back[:].rearrange("p (m j) -> p m j", m=ROW_TILES)
-
+        hp_flipped = act_grouped["hh"][:].rearrange("p (g b u e) -> p g u e b", g=PASSES, u=2, e=2)
         hp_by_tile = act_rows["hh"][:].rearrange("p (m k) -> p m k", m=ROW_TILES)
         out_by_tile = out.rearrange("(m p) j -> p m j", p=P)
+        step = {}
 
-        def blend(t, new_back, update_back):
-            cols = slice(t * P, (t + 1) * P)
-            diff = gates.tile([P, ROW_TILES, P], F32)
-            nc.vector.tensor_tensor(out=diff[:], in0=hp_by_tile[:, :, cols], in1=new_back, op=ALU.subtract)
-            step = gates.tile([P, ROW_TILES, P], F32)
-            nc.vector.scalar_tensor_tensor(
-                out=step[:], in0=update_back, scalar=-1.0, in1=diff[:], op0=ALU.add, op1=ALU.mult
-            )
-            result = gates.tile([P, ROW_TILES, P], F32)
-            nc.vector.tensor_tensor(out=result[:], in0=hp_by_tile[:, :, cols], in1=step[:], op=ALU.add)
+        def flip_back(c):
+            banks = []
+            for half in range(2):
+                back = psum.tile([P, BATCH], F32, tag="bank")
+                banks.append(back)
+            for e in range(2):
+                for m in range(ROW_TILES):
+                    place = (2 * (m % 2) + e) * P
+                    nc.tensor.transpose(
+                        banks[m // 2][:, place : place + P], step[2 * c + e][:, m * P : (m + 1) * P], ident[:]
+                    )
+            return banks
+
+        def add_back(c, banks):
+            cols = slice(c * 2 * P, (c + 1) * 2 * P)
+            result = gates.tile([P, ROW_TILES, 2 * P], F32)
+            for half in range(2):
+                tiles = slice(2 * half, 2 * half + 2)
+                nc.vector.tensor_tensor(
+                    out=result[:, tiles, :].rearrange("p m (j e) -> p m j e", e=2),
+                    in0=hp_by_tile[:, tiles, cols].rearrange("p m (j e) -> p m j e", e=2),
+                    in1=banks[half][:].rearrange("p (m e j) -> p m j e", m=2, e=2),
+                    op=ALU.add,
+                )
             nc.sync.dma_start(out=out_by_tile[:, :, cols], in_=result[:])
 
-        def bias_column(index):
-            return bias[:, index : index + 1]
-
         quantise_weight_blocks(0, range(len(BLOCKS)))
-        new = {}
-        update = {}
         for t in range(COL_TILES):
+            c, e = divmod(t, 2)
+            g, u = divmod(c, 2)
+            pair_done = e == 0 and c > 0
+
             acc_r = multiply(t, GATE_R, ("ih", "hh"))
             reset = gates.tile([P, BATCH], F32)
-            nc.scalar.activation(out=reset[:], in_=acc_r[:], func=ACT.Sigmoid, bias=bias_column(8 * GATE_R + t))
+            nc.scalar.activation(
+                out=reset[:], in_=acc_r[:], func=ACT.Sigmoid, bias=bias[:, e, 4 * GATE_R + c : 4 * GATE_R + c + 1]
+            )
             acc_hn = multiply(t, GATE_N, ("hh",))
             gated = gates.tile([P, BATCH], F32)
             nc.vector.scalar_tensor_tensor(
-                out=gated[:], in0=acc_hn[:], scalar=bias_column(24 + t), in1=reset[:], op0=ALU.add, op1=ALU.mult
+                out=gated[:], in0=acc_hn[:], scalar=bias[:, e, 12 + c : 13 + c], in1=reset[:], op0=ALU.add, op1=ALU.mult
             )
 
             if t + 1 < COL_TILES:
                 quantise_weight_blocks(t + 1, range(0, HALF))
-            if t > 0:
-                new_back = flip_back(new[t - 1])
-                update_back = flip_back(update[t - 1])
+            if pair_done:
+                banks = flip_back(c - 1)
 
             acc_in = multiply(t, GATE_N, ("ih",))
             pre = gates.tile([P, BATCH], F32)
             nc.vector.tensor_tensor(out=pre[:], in0=acc_in[:], in1=gated[:], op=ALU.add)
-            new_t = gates.tile([P, BATCH], F32)
-            nc.scalar.activation(out=new_t[:], in_=pre[:], func=ACT.Tanh, bias=bias_column(8 * GATE_N + t))
-            new[t] = new_t
+            new = gates.tile([P, BATCH], F32)
+            nc.scalar.activation(
+                out=new[:], in_=pre[:], func=ACT.Tanh, bias=bias[:, e, 4 * GATE_N + c : 4 * GATE_N + c + 1]
+            )
             acc_z = multiply(t, GATE_Z, ("ih", "hh"))
-            update_t = gates.tile([P, BATCH], F32)
-            nc.scalar.activation(out=update_t[:], in_=acc_z[:], func=ACT.Sigmoid, bias=bias_column(8 * GATE_Z + t))
-            update[t] = update_t
+            update = gates.tile([P, BATCH], F32)
+            nc.scalar.activation(
+                out=update[:], in_=acc_z[:], func=ACT.Sigmoid, bias=bias[:, e, 4 * GATE_Z + c : 4 * GATE_Z + c + 1]
+            )
 
-            if t > 0:
-                blend(t - 1, new_back, update_back)
+            if pair_done:
+                add_back(c - 1, banks)
+            diff = gates.tile([P, BATCH], F32)
+            nc.vector.tensor_tensor(out=diff[:], in0=hp_flipped[:, g, u, e], in1=new[:], op=ALU.subtract)
+            step_t = gates.tile([P, BATCH], F32)
+            nc.vector.scalar_tensor_tensor(
+                out=step_t[:], in0=update[:], scalar=-1.0, in1=diff[:], op0=ALU.add, op1=ALU.mult
+            )
+            step[t] = step_t
+
             if t + 1 < COL_TILES:
                 quantise_weight_blocks(t + 1, range(HALF, len(BLOCKS)))
 
-        last = COL_TILES - 1
-        new_back = flip_back(new[last])
-        update_back = flip_back(update[last])
-        blend(last, new_back, update_back)
+        banks = flip_back(PAIRS - 1)
+        add_back(PAIRS - 1, banks)

@@ -211,15 +211,15 @@ def tile_prior_pa_kernel(tc, h, prev_rnn_hidden, W_ih, W_hh, b_ih, b_n, out):
             nc.vector.scalar_tensor_tensor(
                 out=gated[:], in0=acc_hn[:], scalar=bias[:, e, 12 + c : 13 + c], in1=reset[:], op0=ALU.add, op1=ALU.mult
             )
+            acc_in = multiply(t, GATE_N, ("ih",))
+            pre = gates.tile([P, BATCH], F32)
+            nc.vector.tensor_tensor(out=pre[:], in0=acc_in[:], in1=gated[:], op=ALU.add)
 
             if t + 1 < COL_TILES:
                 quantise_weight_blocks(t + 1, range(0, HALF))
             if pair_done:
                 banks = flip_back(c - 1)
 
-            acc_in = multiply(t, GATE_N, ("ih",))
-            pre = gates.tile([P, BATCH], F32)
-            nc.vector.tensor_tensor(out=pre[:], in0=acc_in[:], in1=gated[:], op=ALU.add)
             new = gates.tile([P, BATCH], F32)
             nc.scalar.activation(
                 out=new[:], in_=pre[:], func=ACT.Tanh, bias=bias[:, e, 4 * GATE_N + c : 4 * GATE_N + c + 1]

@@ -24,7 +24,6 @@ COL_TILES = R // P
 PAIRS = COL_TILES // 2
 GATE_R, GATE_Z, GATE_N = 0, 1, 2
 BLOCKS = [("ih", GATE_R), ("hh", GATE_R), ("hh", GATE_N), ("ih", GATE_N), ("ih", GATE_Z), ("hh", GATE_Z)]
-HALF = len(BLOCKS) // 2
 BLOCK_WORDS = PASSES * P
 FLOPS = 2 * 2 * BATCH * 3 * R * K
 
@@ -36,10 +35,12 @@ def tile_prior_pa_kernel(tc, h, prev_rnn_hidden, W_ih, W_hh, b_ih, b_n, out):
         const = ctx.enter_context(tc.tile_pool(name="const", bufs=1))
         acts = ctx.enter_context(tc.tile_pool(name="acts", bufs=1))
         rows_pool = ctx.enter_context(tc.tile_pool(name="rows", bufs=COL_TILES))
-        stage = ctx.enter_context(tc.tile_pool(name="stage", bufs=4))
+        stage = ctx.enter_context(tc.tile_pool(name="stage", bufs=6))
         quantised = ctx.enter_context(tc.tile_pool(name="quantised", bufs=2))
         gates = ctx.enter_context(tc.tile_pool(name="gates", bufs=2))
-        psum = ctx.enter_context(tc.psum_pool(name="psum", bufs=8))
+        steps = ctx.enter_context(tc.tile_pool(name="steps", bufs=4))
+        psum = ctx.enter_context(tc.psum_pool(name="psum", bufs=5))
+        accs = ctx.enter_context(tc.psum_pool(name="accs", bufs=3))
 
         bias_rows = const.tile([P, 2 * P], BF16)
         nc.vector.memset(bias_rows[:], 0.0)
@@ -128,33 +129,41 @@ def tile_prior_pa_kernel(tc, h, prev_rnn_hidden, W_ih, W_hh, b_ih, b_n, out):
         w_codes = {}
         w_scales = {}
 
-        def quantise_weight_blocks(t, positions):
+        flipped_blocks = {}
+        grouped_blocks = {}
+
+        def flip_block(t, pos):
+            flipped_blocks[t, pos] = flip(w_rows[t][:].bitcast(F32)[:, pos * WORDS : (pos + 1) * WORDS])
+
+        def regroup_block(t, pos):
+            flipped = flipped_blocks[t, pos]
+            grouped = stage.tile([P, K], BF16, align_bytes=64)
+            nc.scalar.copy(
+                out=grouped[:].bitcast(F32).rearrange("p (g r u) -> p g r u", g=PASSES, u=2),
+                in_=flipped[:].rearrange("p (g u r) -> p g r u", g=PASSES, u=2),
+            )
+            grouped_blocks[t, pos] = grouped
+
+        def quantise_block(t, pos):
             if t not in w_codes:
                 codes = quantised.tile([P, len(BLOCKS) * BLOCK_WORDS], U32, align_bytes=64, tag="w_codes")
                 scales = quantised.tile([P, len(BLOCKS) * BLOCK_WORDS], U8, align_bytes=64, tag="w_scales")
                 w_codes[t] = codes
                 w_scales[t] = scales
-            for pos in positions:
-                flipped = flip(w_rows[t][:].bitcast(F32)[:, pos * WORDS : (pos + 1) * WORDS])
-                grouped = stage.tile([P, K], BF16, align_bytes=64)
-                nc.scalar.copy(
-                    out=grouped[:].bitcast(F32).rearrange("p (g r u) -> p g r u", g=PASSES, u=2),
-                    in_=flipped[:].rearrange("p (g u r) -> p g r u", g=PASSES, u=2),
-                )
-                cols = slice(pos * BLOCK_WORDS, (pos + 1) * BLOCK_WORDS)
-                nc.vector.quantize_mx(
-                    out=w_codes[t][:, cols].bitcast(FP8X4), scales=w_scales[t][:, cols], in_=grouped[:]
-                )
+            cols = slice(pos * BLOCK_WORDS, (pos + 1) * BLOCK_WORDS)
+            nc.vector.quantize_mx(
+                out=w_codes[t][:, cols].bitcast(FP8X4), scales=w_scales[t][:, cols], in_=grouped_blocks[t, pos][:]
+            )
 
         def multiply(t, gate, sources):
-            acc = psum.tile([P, BATCH], F32, tag="bank")
+            total = accs.tile([P, BATCH], F32, tag="acc")
             passes = [(src, g) for src in sources for g in range(PASSES)]
             for i, (src, g) in enumerate(passes):
                 first = BLOCKS.index((src, gate)) * BLOCK_WORDS + g * P
                 w_cols = slice(first, first + P)
                 a_cols = slice(g * BATCH, (g + 1) * BATCH)
                 nc.tensor.matmul_mx(
-                    out=acc[:],
+                    out=total[:],
                     lhsT=w_codes[t][:, w_cols].bitcast(FP8X4),
                     lhsT_scale=w_scales[t][:, w_cols],
                     rhs=act_codes[src][:, a_cols].bitcast(FP8X4),
@@ -162,7 +171,7 @@ def tile_prior_pa_kernel(tc, h, prev_rnn_hidden, W_ih, W_hh, b_ih, b_n, out):
                     start=(i == 0),
                     stop=(i == len(passes) - 1),
                 )
-            return acc
+            return total
 
         hp_flipped = act_grouped["hh"][:].rearrange("p (g b u e) -> p g u e b", g=PASSES, u=2, e=2)
         hp_by_tile = act_rows["hh"][:].rearrange("p (m k) -> p m k", m=ROW_TILES)
@@ -195,53 +204,100 @@ def tile_prior_pa_kernel(tc, h, prev_rnn_hidden, W_ih, W_hh, b_ih, b_n, out):
                 )
             nc.sync.dma_start(out=out_by_tile[:, :, cols], in_=result[:])
 
-        quantise_weight_blocks(0, range(len(BLOCKS)))
-        for t in range(COL_TILES):
-            c, e = divmod(t, 2)
-            g, u = divmod(c, 2)
-            pair_done = e == 0 and c > 0
+        acc = {}
+        made = {}
 
-            acc_r = multiply(t, GATE_R, ("ih", "hh"))
+        def bias_of(t, row):
+            c, e = divmod(t, 2)
+            return bias[:, e, row + c : row + c + 1]
+
+        def reset_gate(t):
             reset = gates.tile([P, BATCH], F32)
-            nc.scalar.activation(
-                out=reset[:], in_=acc_r[:], func=ACT.Sigmoid, bias=bias[:, e, 4 * GATE_R + c : 4 * GATE_R + c + 1]
-            )
-            acc_hn = multiply(t, GATE_N, ("hh",))
+            nc.scalar.activation(out=reset[:], in_=acc[t, "r"][:], func=ACT.Sigmoid, bias=bias_of(t, 4 * GATE_R))
+            made[t, "reset"] = reset
+
+        def gated_sum(t):
             gated = gates.tile([P, BATCH], F32)
             nc.vector.scalar_tensor_tensor(
-                out=gated[:], in0=acc_hn[:], scalar=bias[:, e, 12 + c : 13 + c], in1=reset[:], op0=ALU.add, op1=ALU.mult
+                out=gated[:],
+                in0=acc[t, "hn"][:],
+                scalar=bias_of(t, 12),
+                in1=made[t, "reset"][:],
+                op0=ALU.add,
+                op1=ALU.mult,
             )
-            acc_in = multiply(t, GATE_N, ("ih",))
             pre = gates.tile([P, BATCH], F32)
-            nc.vector.tensor_tensor(out=pre[:], in0=acc_in[:], in1=gated[:], op=ALU.add)
+            nc.vector.tensor_tensor(out=pre[:], in0=acc[t, "in"][:], in1=gated[:], op=ALU.add)
+            made[t, "pre"] = pre
 
-            if t + 1 < COL_TILES:
-                quantise_weight_blocks(t + 1, range(0, HALF))
-            if pair_done:
-                banks = flip_back(c - 1)
-
+        def new_gate(t):
             new = gates.tile([P, BATCH], F32)
-            nc.scalar.activation(
-                out=new[:], in_=pre[:], func=ACT.Tanh, bias=bias[:, e, 4 * GATE_N + c : 4 * GATE_N + c + 1]
-            )
-            acc_z = multiply(t, GATE_Z, ("ih", "hh"))
-            update = gates.tile([P, BATCH], F32)
-            nc.scalar.activation(
-                out=update[:], in_=acc_z[:], func=ACT.Sigmoid, bias=bias[:, e, 4 * GATE_Z + c : 4 * GATE_Z + c + 1]
-            )
+            nc.scalar.activation(out=new[:], in_=made[t, "pre"][:], func=ACT.Tanh, bias=bias_of(t, 4 * GATE_N))
+            made[t, "new"] = new
 
-            if pair_done:
-                add_back(c - 1, banks)
+        def update_gate(t):
+            update = gates.tile([P, BATCH], F32)
+            nc.scalar.activation(out=update[:], in_=acc[t, "z"][:], func=ACT.Sigmoid, bias=bias_of(t, 4 * GATE_Z))
+            made[t, "update"] = update
+
+        def blend_diff(t):
+            c, e = divmod(t, 2)
+            g, u = divmod(c, 2)
             diff = gates.tile([P, BATCH], F32)
-            nc.vector.tensor_tensor(out=diff[:], in0=hp_flipped[:, g, u, e], in1=new[:], op=ALU.subtract)
-            step_t = gates.tile([P, BATCH], F32)
+            nc.vector.tensor_tensor(out=diff[:], in0=hp_flipped[:, g, u, e], in1=made[t, "new"][:], op=ALU.subtract)
+            made[t, "diff"] = diff
+
+        def blend_step(t):
+            step_t = steps.tile([P, BATCH], F32)
             nc.vector.scalar_tensor_tensor(
-                out=step_t[:], in0=update[:], scalar=-1.0, in1=diff[:], op0=ALU.add, op1=ALU.mult
+                out=step_t[:], in0=made[t, "update"][:], scalar=-1.0, in1=made[t, "diff"][:], op0=ALU.add, op1=ALU.mult
             )
             step[t] = step_t
 
-            if t + 1 < COL_TILES:
-                quantise_weight_blocks(t + 1, range(HALF, len(BLOCKS)))
+        for pos in range(len(BLOCKS)):
+            flip_block(0, pos)
+            regroup_block(0, pos)
+            quantise_block(0, pos)
+        for t in range(COL_TILES):
+            c, e = divmod(t, 2)
+            more = t + 1 < COL_TILES
+            if e == 1 and c > 0:
+                banks = flip_back(c - 1)
+                add_back(c - 1, banks)
+            if t > 0:
+                new_gate(t - 1)
+                blend_diff(t - 1)
+            if more:
+                flip_block(t + 1, 0)
+                regroup_block(t + 1, 0)
+                quantise_block(t + 1, 0)
+            if t > 0:
+                update_gate(t - 1)
+                blend_step(t - 1)
+            if more:
+                for pos in range(1, 4):
+                    flip_block(t + 1, pos)
+                    regroup_block(t + 1, pos)
+                    quantise_block(t + 1, pos)
+                flip_block(t + 1, 4)
+                flip_block(t + 1, 5)
+            acc[t, "r"] = multiply(t, GATE_R, ("ih", "hh"))
+            reset_gate(t)
+            if more:
+                regroup_block(t + 1, 4)
+                regroup_block(t + 1, 5)
+            acc[t, "hn"] = multiply(t, GATE_N, ("hh",))
+            acc[t, "in"] = multiply(t, GATE_N, ("ih",))
+            gated_sum(t)
+            if more:
+                quantise_block(t + 1, 4)
+                quantise_block(t + 1, 5)
+            acc[t, "z"] = multiply(t, GATE_Z, ("ih", "hh"))
 
+        t = COL_TILES - 1
+        new_gate(t)
+        blend_diff(t)
+        update_gate(t)
+        blend_step(t)
         banks = flip_back(PAIRS - 1)
         add_back(PAIRS - 1, banks)

@@ -24,6 +24,9 @@ COL_TILES = R // P
 PAIRS = COL_TILES // 2
 GATE_R, GATE_Z, GATE_N = 0, 1, 2
 BLOCKS = [("ih", GATE_R), ("hh", GATE_R), ("hh", GATE_N), ("ih", GATE_N), ("ih", GATE_Z), ("hh", GATE_Z)]
+IH_BLOCKS = [pos for pos, (src, gate) in enumerate(BLOCKS) if src == "ih"]
+HH_BLOCKS = [pos for pos, (src, gate) in enumerate(BLOCKS) if src == "hh"]
+HALF = len(BLOCKS) // 2
 BLOCK_WORDS = PASSES * P
 FLOPS = 2 * 2 * BATCH * 3 * R * K
 
@@ -56,20 +59,31 @@ def tile_prior_pa_kernel(tc, h, prev_rnn_hidden, W_ih, W_hh, b_ih, b_n, out):
         inputs = {"ih": h, "hh": prev_rnn_hidden}
         weights = {"ih": W_ih, "hh": W_hh}
         act_rows = {}
-        for src in ("ih", "hh"):
+        w_rows = []
+
+        def load_activations(src):
             rows = acts.tile([P, ROW_TILES * K], BF16, name="act_rows_" + src)
             act_rows[src] = rows
             for m in range(ROW_TILES):
                 nc.sync.dma_start(out=rows[:, m * K : (m + 1) * K], in_=inputs[src][m * P : (m + 1) * P, :])
-        w_rows = []
+
+        def load_weight_blocks(t, positions):
+            c, e = divmod(t, 2)
+            for pos in positions:
+                src, gate = BLOCKS[pos]
+                first = gate * R + c * 2 * P
+                both = weights[src][first : first + 2 * P, :].rearrange("(p e) k -> p e k", e=2)
+                nc.sync.dma_start(out=w_rows[t][:, pos * K : (pos + 1) * K], in_=both[:, e, :])
+
         for t in range(COL_TILES):
             rows = rows_pool.tile([P, len(BLOCKS) * K], BF16, tag="w_rows", name="w_rows")
             w_rows.append(rows)
-            c, e = divmod(t, 2)
-            for pos, (src, gate) in enumerate(BLOCKS):
-                first = gate * R + c * 2 * P
-                both = weights[src][first : first + 2 * P, :].rearrange("(p e) k -> p e k", e=2)
-                nc.sync.dma_start(out=rows[:, pos * K : (pos + 1) * K], in_=both[:, e, :])
+        load_activations("ih")
+        load_weight_blocks(0, IH_BLOCKS)
+        load_activations("hh")
+        load_weight_blocks(0, HH_BLOCKS)
+        for t in range(1, COL_TILES):
+            load_weight_blocks(t, range(len(BLOCKS)))
 
         def flip(words):
             flipped = psum.tile([P, WORDS], F32, tag="bank")
@@ -83,51 +97,44 @@ def tile_prior_pa_kernel(tc, h, prev_rnn_hidden, W_ih, W_hh, b_ih, b_n, out):
         act_grouped = {}
         for src in ("ih", "hh"):
             grouped = acts.tile([P, PASSES * BATCH * 4], BF16, align_bytes=64, name="act_grouped_" + src)
-            act_grouped[src] = grouped
-            for m in range(ROW_TILES):
-                flipped = flip(act_rows[src][:].bitcast(F32)[:, m * WORDS : (m + 1) * WORDS])
-                copy = nc.scalar.copy if m % 2 == 0 else nc.vector.tensor_copy
-                if src == "ih":
-                    copy(
-                        out=grouped[:]
-                        .bitcast(F32)
-                        .rearrange("p (g m r u) -> p g m r u", g=PASSES, m=ROW_TILES, u=2)[:, :, m],
-                        in_=flipped[:].rearrange("p (g u r) -> p g r u", g=PASSES, u=2),
-                    )
-                else:
-                    for g in range(PASSES):
-                        copy(
-                            out=grouped[:].rearrange(
-                                "p (g m r u e) -> p g m r u e", g=PASSES, m=ROW_TILES, u=2, e=2
-                            )[:, g, m],
-                            in_=flipped[:]
-                            .bitcast(BF16)
-                            .rearrange("p (g u r e) -> p g r u e", g=PASSES, u=2, e=2)[:, g],
-                        )
             codes = acts.tile([P, PASSES * BATCH], U32, align_bytes=64, name="act_codes_" + src)
             scales = acts.tile([P, PASSES * BATCH], U8, align_bytes=64, name="act_scales_" + src)
-            for g in range(PASSES):
-                cols = slice(g * BATCH, (g + 1) * BATCH)
-                nc.vector.quantize_mx(
-                    out=codes[:, cols].bitcast(FP8X4),
-                    scales=scales[:, cols],
-                    in_=grouped[:, 4 * g * BATCH : 4 * (g + 1) * BATCH],
-                )
+            act_grouped[src] = grouped
             act_codes[src] = codes
             act_scales[src] = scales
 
+        def prepare_rows(src, m, copy):
+            flipped = flip(act_rows[src][:].bitcast(F32)[:, m * WORDS : (m + 1) * WORDS])
+            copy(
+                out=act_grouped[src][:]
+                .bitcast(F32)
+                .rearrange("p (g m r u) -> p g m r u", g=PASSES, m=ROW_TILES, u=2)[:, :, m],
+                in_=flipped[:].rearrange("p (g u r) -> p g r u", g=PASSES, u=2),
+            )
+            for g in range(PASSES):
+                first = g * BATCH + m * P
+                cols = slice(first, first + P)
+                nc.vector.quantize_mx(
+                    out=act_codes[src][:, cols].bitcast(FP8X4),
+                    scales=act_scales[src][:, cols],
+                    in_=act_grouped[src][:, 4 * first : 4 * (first + P)],
+                )
+
+        bias = const.tile([P, 2, 16], F32)
         bias_parted = const.tile([P, 2, P], F32)
         nc.vector.tensor_copy(out=bias_parted[:], in_=bias_rows[:].rearrange("r (p e) -> r e p", e=2))
-        bias_bank = psum.tile([P, WORDS], F32, tag="bank")
-        for e in range(2):
-            nc.tensor.transpose(bias_bank[:, e * P : (e + 1) * P], bias_parted[:, e, :], ident[:])
-        bias = const.tile([P, 2, 16], F32)
-        nc.vector.tensor_copy(
-            out=bias[:], in_=bias_bank[:, 0 : 2 * P].rearrange("p (e r) -> p e r", e=2)[:, :, 0:16]
-        )
+
+        def prepare_biases():
+            bias_bank = psum.tile([P, WORDS], F32, tag="bank")
+            for e in range(2):
+                nc.tensor.transpose(bias_bank[:, e * P : (e + 1) * P], bias_parted[:, e, :], ident[:])
+            nc.vector.tensor_copy(
+                out=bias[:], in_=bias_bank[:, 0 : 2 * P].rearrange("p (e r) -> p e r", e=2)[:, :, 0:16]
+            )
 
         w_codes = {}
         w_scales = {}
+        acc = {}
 
         flipped_blocks = {}
         grouped_blocks = {}
@@ -135,10 +142,10 @@ def tile_prior_pa_kernel(tc, h, prev_rnn_hidden, W_ih, W_hh, b_ih, b_n, out):
         def flip_block(t, pos):
             flipped_blocks[t, pos] = flip(w_rows[t][:].bitcast(F32)[:, pos * WORDS : (pos + 1) * WORDS])
 
-        def regroup_block(t, pos):
+        def regroup_block(t, pos, copy=nc.scalar.copy):
             flipped = flipped_blocks[t, pos]
             grouped = stage.tile([P, K], BF16, align_bytes=64)
-            nc.scalar.copy(
+            copy(
                 out=grouped[:].bitcast(F32).rearrange("p (g r u) -> p g r u", g=PASSES, u=2),
                 in_=flipped[:].rearrange("p (g u r) -> p g r u", g=PASSES, u=2),
             )
@@ -155,8 +162,7 @@ def tile_prior_pa_kernel(tc, h, prev_rnn_hidden, W_ih, W_hh, b_ih, b_n, out):
                 out=w_codes[t][:, cols].bitcast(FP8X4), scales=w_scales[t][:, cols], in_=grouped_blocks[t, pos][:]
             )
 
-        def multiply(t, gate, sources):
-            total = accs.tile([P, BATCH], F32, tag="acc")
+        def multiply(total, t, gate, sources, start=True, stop=True):
             passes = [(src, g) for src in sources for g in range(PASSES)]
             for i, (src, g) in enumerate(passes):
                 first = BLOCKS.index((src, gate)) * BLOCK_WORDS + g * P
@@ -168,9 +174,13 @@ def tile_prior_pa_kernel(tc, h, prev_rnn_hidden, W_ih, W_hh, b_ih, b_n, out):
                     lhsT_scale=w_scales[t][:, w_cols],
                     rhs=act_codes[src][:, a_cols].bitcast(FP8X4),
                     rhs_scale=act_scales[src][:, a_cols],
-                    start=(i == 0),
-                    stop=(i == len(passes) - 1),
+                    start=start and i == 0,
+                    stop=stop and i == len(passes) - 1,
                 )
+
+        def new_sum(t, part):
+            total = accs.tile([P, BATCH], F32, tag="acc")
+            acc[t, part] = total
             return total
 
         hp_flipped = act_grouped["hh"][:].rearrange("p (g b u e) -> p g u e b", g=PASSES, u=2, e=2)
@@ -204,7 +214,6 @@ def tile_prior_pa_kernel(tc, h, prev_rnn_hidden, W_ih, W_hh, b_ih, b_n, out):
                 )
             nc.sync.dma_start(out=out_by_tile[:, :, cols], in_=result[:])
 
-        acc = {}
         made = {}
 
         def bias_of(t, row):
@@ -254,45 +263,69 @@ def tile_prior_pa_kernel(tc, h, prev_rnn_hidden, W_ih, W_hh, b_ih, b_n, out):
             )
             step[t] = step_t
 
-        for pos in range(len(BLOCKS)):
+        for m in range(ROW_TILES):
+            prepare_rows("ih", m, nc.scalar.copy)
+            if m == 1:
+                prepare_biases()
+        for pos in IH_BLOCKS:
             flip_block(0, pos)
             regroup_block(0, pos)
             quantise_block(0, pos)
-        for t in range(COL_TILES):
+        prepare_rows("hh", 0, nc.scalar.copy)
+        prepare_rows("hh", 1, nc.vector.tensor_copy)
+        multiply(new_sum(0, "r"), 0, GATE_R, ("ih",), stop=False)
+        multiply(new_sum(0, "in"), 0, GATE_N, ("ih",))
+        multiply(new_sum(0, "z"), 0, GATE_Z, ("ih",), stop=False)
+        for m in range(2, ROW_TILES):
+            prepare_rows("hh", m, nc.scalar.copy if m % 2 == 0 else nc.vector.tensor_copy)
+        for i, block in enumerate([(0, pos) for pos in HH_BLOCKS] + [(1, 0), (1, 1)]):
+            flip_block(*block)
+            regroup_block(*block, copy=nc.scalar.copy if i % 2 == 0 else nc.vector.tensor_copy)
+            quantise_block(*block)
+        multiply(acc[0, "r"], 0, GATE_R, ("hh",), start=False)
+        reset_gate(0)
+        total = psum.tile([P, WORDS], F32, tag="bank")
+        acc[0, "hn"] = total
+        multiply(total, 0, GATE_N, ("hh",))
+        gated_sum(0)
+        multiply(acc[0, "z"], 0, GATE_Z, ("hh",), start=False)
+
+        ahead = 2
+        for t in range(1, COL_TILES):
             c, e = divmod(t, 2)
-            more = t + 1 < COL_TILES
+            run = [(t, pos) for pos in range(ahead, len(BLOCKS))]
+            if t + 1 < COL_TILES:
+                run += [(t + 1, pos) for pos in range(HALF)]
+            ahead = HALF
             if e == 1 and c > 0:
                 banks = flip_back(c - 1)
                 add_back(c - 1, banks)
-            if t > 0:
+            if t > 1:
                 new_gate(t - 1)
                 blend_diff(t - 1)
-            if more:
-                flip_block(t + 1, 0)
-                regroup_block(t + 1, 0)
-                quantise_block(t + 1, 0)
-            if t > 0:
-                update_gate(t - 1)
-                blend_step(t - 1)
-            if more:
-                for pos in range(1, 4):
-                    flip_block(t + 1, pos)
-                    regroup_block(t + 1, pos)
-                    quantise_block(t + 1, pos)
-                flip_block(t + 1, 4)
-                flip_block(t + 1, 5)
-            acc[t, "r"] = multiply(t, GATE_R, ("ih", "hh"))
+            late = run[4:]
+            for i, block in enumerate(run[:4]):
+                flip_block(*block)
+                regroup_block(*block)
+                quantise_block(*block)
+                if i == 1 and t == 1:
+                    new_gate(t - 1)
+                    blend_diff(t - 1)
+                if i == (2 if t == 1 else 0):
+                    update_gate(t - 1)
+                    blend_step(t - 1)
+            for block in late:
+                flip_block(*block)
+            multiply(new_sum(t, "r"), t, GATE_R, ("ih", "hh"))
             reset_gate(t)
-            if more:
-                regroup_block(t + 1, 4)
-                regroup_block(t + 1, 5)
-            acc[t, "hn"] = multiply(t, GATE_N, ("hh",))
-            acc[t, "in"] = multiply(t, GATE_N, ("ih",))
+            for block in late:
+                regroup_block(*block)
+            multiply(new_sum(t, "hn"), t, GATE_N, ("hh",))
+            multiply(new_sum(t, "in"), t, GATE_N, ("ih",))
             gated_sum(t)
-            if more:
-                quantise_block(t + 1, 4)
-                quantise_block(t + 1, 5)
-            acc[t, "z"] = multiply(t, GATE_Z, ("ih", "hh"))
+            for block in late:
+                quantise_block(*block)
+            multiply(new_sum(t, "z"), t, GATE_Z, ("ih", "hh"))
 
         t = COL_TILES - 1
         new_gate(t)

@@ -24,9 +24,9 @@ COL_TILES = R // P
 PAIRS = COL_TILES // 2
 GATE_R, GATE_Z, GATE_N = 0, 1, 2
 BLOCKS = [("ih", GATE_R), ("hh", GATE_R), ("hh", GATE_N), ("ih", GATE_N), ("ih", GATE_Z), ("hh", GATE_Z)]
+BLOCK_PAIRS = len(BLOCKS) // 2
 IH_BLOCKS = [pos for pos, (src, gate) in enumerate(BLOCKS) if src == "ih"]
 HH_BLOCKS = [pos for pos, (src, gate) in enumerate(BLOCKS) if src == "hh"]
-HALF = len(BLOCKS) // 2
 BLOCK_WORDS = PASSES * P
 FLOPS = 2 * 2 * BATCH * 3 * R * K
 
@@ -38,12 +38,11 @@ def tile_prior_pa_kernel(tc, h, prev_rnn_hidden, W_ih, W_hh, b_ih, b_n, out):
         const = ctx.enter_context(tc.tile_pool(name="const", bufs=1))
         acts = ctx.enter_context(tc.tile_pool(name="acts", bufs=1))
         rows_pool = ctx.enter_context(tc.tile_pool(name="rows", bufs=COL_TILES))
-        stage = ctx.enter_context(tc.tile_pool(name="stage", bufs=6))
+        stage = ctx.enter_context(tc.tile_pool(name="stage", bufs=4))
         quantised = ctx.enter_context(tc.tile_pool(name="quantised", bufs=2))
         gates = ctx.enter_context(tc.tile_pool(name="gates", bufs=2))
         steps = ctx.enter_context(tc.tile_pool(name="steps", bufs=4))
-        psum = ctx.enter_context(tc.psum_pool(name="psum", bufs=5))
-        accs = ctx.enter_context(tc.psum_pool(name="accs", bufs=3))
+        psum = ctx.enter_context(tc.psum_pool(name="psum", bufs=8))
 
         bias_rows = const.tile([P, 2 * P], BF16)
         nc.vector.memset(bias_rows[:], 0.0)
@@ -60,6 +59,9 @@ def tile_prior_pa_kernel(tc, h, prev_rnn_hidden, W_ih, W_hh, b_ih, b_n, out):
         weights = {"ih": W_ih, "hh": W_hh}
         act_rows = {}
         w_rows = []
+        for t in range(COL_TILES):
+            rows = rows_pool.tile([P, len(BLOCKS) * K], BF16, tag="w_rows", name="w_rows")
+            w_rows.append(rows)
 
         def load_activations(src):
             rows = acts.tile([P, ROW_TILES * K], BF16, name="act_rows_" + src)
@@ -75,9 +77,6 @@ def tile_prior_pa_kernel(tc, h, prev_rnn_hidden, W_ih, W_hh, b_ih, b_n, out):
                 both = weights[src][first : first + 2 * P, :].rearrange("(p e) k -> p e k", e=2)
                 nc.sync.dma_start(out=w_rows[t][:, pos * K : (pos + 1) * K], in_=both[:, e, :])
 
-        for t in range(COL_TILES):
-            rows = rows_pool.tile([P, len(BLOCKS) * K], BF16, tag="w_rows", name="w_rows")
-            w_rows.append(rows)
         load_activations("ih")
         load_weight_blocks(0, IH_BLOCKS)
         load_activations("hh")
@@ -92,11 +91,17 @@ def tile_prior_pa_kernel(tc, h, prev_rnn_hidden, W_ih, W_hh, b_ih, b_n, out):
                 nc.tensor.transpose(flipped[:, cols], words[:, cols], ident[:])
             return flipped
 
+        def regroup(copy, grouped, flipped):
+            copy(
+                out=grouped.bitcast(F32).rearrange("p (g r u) -> p g r u", g=PASSES, u=2),
+                in_=flipped[:].rearrange("p (g u r) -> p g r u", g=PASSES, u=2),
+            )
+
         act_codes = {}
         act_scales = {}
         act_grouped = {}
         for src in ("ih", "hh"):
-            grouped = acts.tile([P, PASSES * BATCH * 4], BF16, align_bytes=64, name="act_grouped_" + src)
+            grouped = acts.tile([P, ROW_TILES * 4 * PASSES * P], BF16, align_bytes=64, name="act_grouped_" + src)
             codes = acts.tile([P, PASSES * BATCH], U32, align_bytes=64, name="act_codes_" + src)
             scales = acts.tile([P, PASSES * BATCH], U8, align_bytes=64, name="act_scales_" + src)
             act_grouped[src] = grouped
@@ -105,26 +110,24 @@ def tile_prior_pa_kernel(tc, h, prev_rnn_hidden, W_ih, W_hh, b_ih, b_n, out):
 
         def prepare_rows(src, m, copy):
             flipped = flip(act_rows[src][:].bitcast(F32)[:, m * WORDS : (m + 1) * WORDS])
-            copy(
-                out=act_grouped[src][:]
-                .bitcast(F32)
-                .rearrange("p (g m r u) -> p g m r u", g=PASSES, m=ROW_TILES, u=2)[:, :, m],
-                in_=flipped[:].rearrange("p (g u r) -> p g r u", g=PASSES, u=2),
-            )
+            grouped = act_grouped[src][:, m * K : (m + 1) * K]
+            regroup(copy, grouped, flipped)
             for g in range(PASSES):
-                first = g * BATCH + m * P
-                cols = slice(first, first + P)
+                cols = slice(g * BATCH + m * P, g * BATCH + (m + 1) * P)
                 nc.vector.quantize_mx(
                     out=act_codes[src][:, cols].bitcast(FP8X4),
                     scales=act_scales[src][:, cols],
-                    in_=act_grouped[src][:, 4 * first : 4 * (first + P)],
+                    in_=grouped[:, g * 4 * P : (g + 1) * 4 * P],
                 )
 
         bias = const.tile([P, 2, 16], F32)
-        bias_parted = const.tile([P, 2, P], F32)
-        nc.vector.tensor_copy(out=bias_parted[:], in_=bias_rows[:].rearrange("r (p e) -> r e p", e=2))
 
-        def prepare_biases():
+        bias_parted = const.tile([P, 2, P], F32)
+
+        def part_biases():
+            nc.vector.tensor_copy(out=bias_parted[:], in_=bias_rows[:].rearrange("r (p e) -> r e p", e=2))
+
+        def transpose_biases():
             bias_bank = psum.tile([P, WORDS], F32, tag="bank")
             for e in range(2):
                 nc.tensor.transpose(bias_bank[:, e * P : (e + 1) * P], bias_parted[:, e, :], ident[:])
@@ -132,37 +135,40 @@ def tile_prior_pa_kernel(tc, h, prev_rnn_hidden, W_ih, W_hh, b_ih, b_n, out):
                 out=bias[:], in_=bias_bank[:, 0 : 2 * P].rearrange("p (e r) -> p e r", e=2)[:, :, 0:16]
             )
 
-        w_codes = {}
-        w_scales = {}
-        acc = {}
+        def bias_of(t, row):
+            c, e = divmod(t, 2)
+            return bias[:, e, row + c : row + c + 1]
 
+        w_codes = []
+        w_scales = []
         flipped_blocks = {}
-        grouped_blocks = {}
+        grouped_pairs = {}
 
         def flip_block(t, pos):
-            flipped_blocks[t, pos] = flip(w_rows[t][:].bitcast(F32)[:, pos * WORDS : (pos + 1) * WORDS])
+            flipped_blocks[pos] = flip(w_rows[t][:].bitcast(F32)[:, pos * WORDS : (pos + 1) * WORDS])
 
-        def regroup_block(t, pos, copy=nc.scalar.copy):
-            flipped = flipped_blocks[t, pos]
-            grouped = stage.tile([P, K], BF16, align_bytes=64)
-            copy(
-                out=grouped[:].bitcast(F32).rearrange("p (g r u) -> p g r u", g=PASSES, u=2),
-                in_=flipped[:].rearrange("p (g u r) -> p g r u", g=PASSES, u=2),
-            )
-            grouped_blocks[t, pos] = grouped
+        def regroup_block(pos, copy=nc.scalar.copy):
+            if pos // 2 not in grouped_pairs:
+                grouped = stage.tile([P, 2 * K], BF16, align_bytes=64)
+                grouped_pairs[pos // 2] = grouped
+            half = slice(pos % 2 * K, (pos % 2 + 1) * K)
+            regroup(copy, grouped_pairs[pos // 2][:, half], flipped_blocks.pop(pos))
 
-        def quantise_block(t, pos):
-            if t not in w_codes:
-                codes = quantised.tile([P, len(BLOCKS) * BLOCK_WORDS], U32, align_bytes=64, tag="w_codes")
-                scales = quantised.tile([P, len(BLOCKS) * BLOCK_WORDS], U8, align_bytes=64, tag="w_scales")
-                w_codes[t] = codes
-                w_scales[t] = scales
-            cols = slice(pos * BLOCK_WORDS, (pos + 1) * BLOCK_WORDS)
-            nc.vector.quantize_mx(
-                out=w_codes[t][:, cols].bitcast(FP8X4), scales=w_scales[t][:, cols], in_=grouped_blocks[t, pos][:]
-            )
+        def new_codes():
+            codes = quantised.tile([P, len(BLOCKS) * BLOCK_WORDS], U32, align_bytes=64, tag="w_codes")
+            scales = quantised.tile([P, len(BLOCKS) * BLOCK_WORDS], U8, align_bytes=64, tag="w_scales")
+            w_codes.append(codes)
+            w_scales.append(scales)
 
-        def multiply(total, t, gate, sources, start=True, stop=True):
+        def quantise(t, first, last, grouped):
+            cols = slice(first * BLOCK_WORDS, last * BLOCK_WORDS)
+            nc.vector.quantize_mx(out=w_codes[t][:, cols].bitcast(FP8X4), scales=w_scales[t][:, cols], in_=grouped)
+
+        def quantise_pair(t, q):
+            quantise(t, 2 * q, 2 * q + 2, grouped_pairs.pop(q)[:])
+
+        def multiply(t, gate, sources):
+            total = psum.tile([P, BATCH], F32, tag="bank")
             passes = [(src, g) for src in sources for g in range(PASSES)]
             for i, (src, g) in enumerate(passes):
                 first = BLOCKS.index((src, gate)) * BLOCK_WORDS + g * P
@@ -174,163 +180,212 @@ def tile_prior_pa_kernel(tc, h, prev_rnn_hidden, W_ih, W_hh, b_ih, b_n, out):
                     lhsT_scale=w_scales[t][:, w_cols],
                     rhs=act_codes[src][:, a_cols].bitcast(FP8X4),
                     rhs_scale=act_scales[src][:, a_cols],
-                    start=start and i == 0,
-                    stop=stop and i == len(passes) - 1,
+                    start=(i == 0),
+                    stop=(i == len(passes) - 1),
                 )
-
-        def new_sum(t, part):
-            total = accs.tile([P, BATCH], F32, tag="acc")
-            acc[t, part] = total
             return total
 
-        hp_flipped = act_grouped["hh"][:].rearrange("p (g b u e) -> p g u e b", g=PASSES, u=2, e=2)
+        hp_flipped = act_grouped["hh"][:].rearrange(
+            "p (m g r u e) -> p g u e m r", m=ROW_TILES, g=PASSES, u=2, e=2
+        )
+        sums = {}
+        gate_tiles = {}
+        step = {}
+        ALL = slice(0, ROW_TILES)
+
+        def gate_tile(name):
+            made = gates.tile([P, BATCH], F32, tag=name, name=name)
+            gate_tiles[name] = made
+
+        def rows_of(tiles):
+            return slice(tiles.start * P, tiles.stop * P)
+
+        def reset_gate(t, tiles=ALL):
+            rows = rows_of(tiles)
+            nc.scalar.activation(
+                out=gate_tiles["reset"][:, rows], in_=sums["r"][:, rows], func=ACT.Sigmoid, bias=bias_of(t, 4 * GATE_R)
+            )
+
+        def gated_sum(t, tiles=ALL):
+            rows = rows_of(tiles)
+            nc.vector.scalar_tensor_tensor(
+                out=gate_tiles["gated"][:, rows],
+                in0=sums["hn"][:, rows],
+                scalar=bias_of(t, 12),
+                in1=gate_tiles["reset"][:, rows],
+                op0=ALU.add,
+                op1=ALU.mult,
+            )
+
+        def before_tanh(t, tiles=ALL):
+            rows = rows_of(tiles)
+            nc.vector.tensor_tensor(
+                out=gate_tiles["pre"][:, rows], in0=sums["in"][:, rows], in1=gate_tiles["gated"][:, rows], op=ALU.add
+            )
+
+        def new_gate(t, tiles=ALL):
+            rows = rows_of(tiles)
+            nc.scalar.activation(
+                out=gate_tiles["new"][:, rows], in_=gate_tiles["pre"][:, rows], func=ACT.Tanh, bias=bias_of(t, 4 * GATE_N)
+            )
+
+        def update_gate(t, tiles=ALL):
+            rows = rows_of(tiles)
+            nc.scalar.activation(
+                out=gate_tiles["update"][:, rows], in_=sums["z"][:, rows], func=ACT.Sigmoid, bias=bias_of(t, 4 * GATE_Z)
+            )
+
+        def blend_diff(t, tiles=ALL):
+            if tiles.start == 0:
+                gate_tile("diff")
+            rows = rows_of(tiles)
+            c, e = divmod(t, 2)
+            g, u = divmod(c, 2)
+            nc.vector.tensor_tensor(
+                out=gate_tiles["diff"][:, rows].rearrange("p (m r) -> p m r", r=P),
+                in0=hp_flipped[:, g, u, e, tiles],
+                in1=gate_tiles["new"][:, rows].rearrange("p (m r) -> p m r", r=P),
+                op=ALU.subtract,
+            )
+
+        def blend_step(t, tiles=ALL):
+            if t not in step:
+                step_t = steps.tile([P, BATCH], F32)
+                step[t] = step_t
+            rows = rows_of(tiles)
+            nc.vector.scalar_tensor_tensor(
+                out=step[t][:, rows],
+                in0=gate_tiles["update"][:, rows],
+                scalar=-1.0,
+                in1=gate_tiles["diff"][:, rows],
+                op0=ALU.add,
+                op1=ALU.mult,
+            )
+
         hp_by_tile = act_rows["hh"][:].rearrange("p (m k) -> p m k", m=ROW_TILES)
         out_by_tile = out.rearrange("(m p) j -> p m j", p=P)
-        step = {}
 
-        def flip_back(c):
+        def new_back():
             banks = []
             for half in range(2):
                 back = psum.tile([P, BATCH], F32, tag="bank")
                 banks.append(back)
-            for e in range(2):
-                for m in range(ROW_TILES):
-                    place = (2 * (m % 2) + e) * P
-                    nc.tensor.transpose(
-                        banks[m // 2][:, place : place + P], step[2 * c + e][:, m * P : (m + 1) * P], ident[:]
-                    )
             return banks
 
-        def add_back(c, banks):
+        def flip_back(banks, t, tiles=ALL):
+            for m in range(tiles.start, tiles.stop):
+                place = (2 * (m % 2) + t % 2) * P
+                nc.tensor.transpose(banks[m // 2][:, place : place + P], step[t][:, m * P : (m + 1) * P], ident[:])
+
+        def add_back(result, banks, c, half):
+            tiles = slice(2 * half, 2 * half + 2)
             cols = slice(c * 2 * P, (c + 1) * 2 * P)
-            result = gates.tile([P, ROW_TILES, 2 * P], F32)
-            for half in range(2):
-                tiles = slice(2 * half, 2 * half + 2)
-                nc.vector.tensor_tensor(
-                    out=result[:, tiles, :].rearrange("p m (j e) -> p m j e", e=2),
-                    in0=hp_by_tile[:, tiles, cols].rearrange("p m (j e) -> p m j e", e=2),
-                    in1=banks[half][:].rearrange("p (m e j) -> p m j e", m=2, e=2),
-                    op=ALU.add,
-                )
-            nc.sync.dma_start(out=out_by_tile[:, :, cols], in_=result[:])
-
-        made = {}
-
-        def bias_of(t, row):
-            c, e = divmod(t, 2)
-            return bias[:, e, row + c : row + c + 1]
-
-        def reset_gate(t):
-            reset = gates.tile([P, BATCH], F32)
-            nc.scalar.activation(out=reset[:], in_=acc[t, "r"][:], func=ACT.Sigmoid, bias=bias_of(t, 4 * GATE_R))
-            made[t, "reset"] = reset
-
-        def gated_sum(t):
-            gated = gates.tile([P, BATCH], F32)
-            nc.vector.scalar_tensor_tensor(
-                out=gated[:],
-                in0=acc[t, "hn"][:],
-                scalar=bias_of(t, 12),
-                in1=made[t, "reset"][:],
-                op0=ALU.add,
-                op1=ALU.mult,
+            nc.vector.tensor_tensor(
+                out=result[:, tiles, :].rearrange("p m (j e) -> p m j e", e=2),
+                in0=hp_by_tile[:, tiles, cols].rearrange("p m (j e) -> p m j e", e=2),
+                in1=banks[half][:].rearrange("p (m e j) -> p m j e", m=2, e=2),
+                op=ALU.add,
             )
-            pre = gates.tile([P, BATCH], F32)
-            nc.vector.tensor_tensor(out=pre[:], in0=acc[t, "in"][:], in1=gated[:], op=ALU.add)
-            made[t, "pre"] = pre
 
-        def new_gate(t):
-            new = gates.tile([P, BATCH], F32)
-            nc.scalar.activation(out=new[:], in_=made[t, "pre"][:], func=ACT.Tanh, bias=bias_of(t, 4 * GATE_N))
-            made[t, "new"] = new
-
-        def update_gate(t):
-            update = gates.tile([P, BATCH], F32)
-            nc.scalar.activation(out=update[:], in_=acc[t, "z"][:], func=ACT.Sigmoid, bias=bias_of(t, 4 * GATE_Z))
-            made[t, "update"] = update
-
-        def blend_diff(t):
-            c, e = divmod(t, 2)
-            g, u = divmod(c, 2)
-            diff = gates.tile([P, BATCH], F32)
-            nc.vector.tensor_tensor(out=diff[:], in0=hp_flipped[:, g, u, e], in1=made[t, "new"][:], op=ALU.subtract)
-            made[t, "diff"] = diff
-
-        def blend_step(t):
-            step_t = steps.tile([P, BATCH], F32)
-            nc.vector.scalar_tensor_tensor(
-                out=step_t[:], in0=made[t, "update"][:], scalar=-1.0, in1=made[t, "diff"][:], op0=ALU.add, op1=ALU.mult
-            )
-            step[t] = step_t
+        def store(result, c, tiles):
+            cols = slice(c * 2 * P, (c + 1) * 2 * P)
+            nc.sync.dma_start(out=out_by_tile[:, tiles, cols], in_=result[:, tiles, :])
 
         for m in range(ROW_TILES):
             prepare_rows("ih", m, nc.scalar.copy)
-            if m == 1:
-                prepare_biases()
+        part_biases()
+        new_codes()
         for pos in IH_BLOCKS:
             flip_block(0, pos)
-            regroup_block(0, pos)
-            quantise_block(0, pos)
-        prepare_rows("hh", 0, nc.scalar.copy)
-        prepare_rows("hh", 1, nc.vector.tensor_copy)
-        multiply(new_sum(0, "r"), 0, GATE_R, ("ih",), stop=False)
-        multiply(new_sum(0, "in"), 0, GATE_N, ("ih",))
-        multiply(new_sum(0, "z"), 0, GATE_Z, ("ih",), stop=False)
-        for m in range(2, ROW_TILES):
+            regroup_block(pos)
+            quantise(0, pos, pos + 1, grouped_pairs[pos // 2][:, pos % 2 * K : (pos % 2 + 1) * K])
+        for m in range(ROW_TILES):
             prepare_rows("hh", m, nc.scalar.copy if m % 2 == 0 else nc.vector.tensor_copy)
-        for i, block in enumerate([(0, pos) for pos in HH_BLOCKS] + [(1, 0), (1, 1)]):
-            flip_block(*block)
-            regroup_block(*block, copy=nc.scalar.copy if i % 2 == 0 else nc.vector.tensor_copy)
-            quantise_block(*block)
-        multiply(acc[0, "r"], 0, GATE_R, ("hh",), start=False)
-        reset_gate(0)
-        total = psum.tile([P, WORDS], F32, tag="bank")
-        acc[0, "hn"] = total
-        multiply(total, 0, GATE_N, ("hh",))
-        gated_sum(0)
-        multiply(acc[0, "z"], 0, GATE_Z, ("hh",), start=False)
+            if m == 1:
+                transpose_biases()
+        for i, pos in enumerate(HH_BLOCKS):
+            flip_block(0, pos)
+            regroup_block(pos, nc.scalar.copy if i % 2 == 0 else nc.vector.tensor_copy)
+            quantise(0, pos, pos + 1, grouped_pairs[pos // 2][:, pos % 2 * K : (pos % 2 + 1) * K])
+        grouped_pairs.clear()
 
-        ahead = 2
-        for t in range(1, COL_TILES):
+        for t in range(COL_TILES):
             c, e = divmod(t, 2)
-            run = [(t, pos) for pos in range(ahead, len(BLOCKS))]
-            if t + 1 < COL_TILES:
-                run += [(t + 1, pos) for pos in range(HALF)]
-            ahead = HALF
+            more = t + 1 < COL_TILES
+            done = t - 1
+            if more:
+                new_codes()
             if e == 1 and c > 0:
-                banks = flip_back(c - 1)
-                add_back(c - 1, banks)
-            if t > 1:
-                new_gate(t - 1)
-                blend_diff(t - 1)
-            late = run[4:]
-            for i, block in enumerate(run[:4]):
-                flip_block(*block)
-                regroup_block(*block)
-                quantise_block(*block)
-                if i == 1 and t == 1:
-                    new_gate(t - 1)
-                    blend_diff(t - 1)
-                if i == (2 if t == 1 else 0):
-                    update_gate(t - 1)
-                    blend_step(t - 1)
-            for block in late:
-                flip_block(*block)
-            multiply(new_sum(t, "r"), t, GATE_R, ("ih", "hh"))
-            reset_gate(t)
-            for block in late:
-                regroup_block(*block)
-            multiply(new_sum(t, "hn"), t, GATE_N, ("hh",))
-            multiply(new_sum(t, "in"), t, GATE_N, ("ih",))
-            gated_sum(t)
-            for block in late:
-                quantise_block(*block)
-            multiply(new_sum(t, "z"), t, GATE_Z, ("ih", "hh"))
+                banks = new_back()
+                flip_back(banks, t - 3)
+                flip_back(banks, t - 2)
+                result = gates.tile([P, ROW_TILES, 2 * P], F32)
+                add_back(result, banks, c - 1, 0)
+                add_back(result, banks, c - 1, 1)
+                store(result, c - 1, ALL)
+            if done >= 0:
+                gate_tile("update")
+                update_gate(done)
+            if more:
+                flip_block(t + 1, 0)
+                regroup_block(0)
+            if done >= 0:
+                gate_tile("new")
+                new_gate(done)
+            if done >= 0 and more:
+                blend_diff(done)
+            if more:
+                flip_block(t + 1, 1)
+                regroup_block(1)
+                quantise_pair(t + 1, 0)
+            if done >= 0 and more:
+                blend_step(done)
+            if more:
+                flip_block(t + 1, 2)
+                regroup_block(2)
+                flip_block(t + 1, 3)
+                regroup_block(3)
+                quantise_pair(t + 1, 1)
+                flip_block(t + 1, 4)
+                flip_block(t + 1, 5)
+            sums["r"] = multiply(t, GATE_R, ("ih", "hh"))
+            gate_tile("reset")
+            gate_tile("gated")
+            gate_tile("pre")
+            halves = [ALL] if more else [slice(0, 2), slice(2, 4)]
+            for tiles in halves:
+                reset_gate(t, tiles)
+            if more:
+                regroup_block(4)
+                regroup_block(5)
+            sums["hn"] = multiply(t, GATE_N, ("hh",))
+            for tiles in halves:
+                gated_sum(t, tiles)
+            sums["in"] = multiply(t, GATE_N, ("ih",))
+            for tiles in halves:
+                before_tanh(t, tiles)
+            if not more:
+                blend_diff(done)
+                blend_step(done)
+            if more:
+                quantise_pair(t + 1, 2)
+            sums["z"] = multiply(t, GATE_Z, ("ih", "hh"))
 
         t = COL_TILES - 1
-        new_gate(t)
-        blend_diff(t)
-        update_gate(t)
-        blend_step(t)
-        banks = flip_back(PAIRS - 1)
-        add_back(PAIRS - 1, banks)
+        banks = new_back()
+        flip_back(banks, t - 1)
+        gate_tile("update")
+        gate_tile("new")
+        for tiles in halves:
+            new_gate(t, tiles)
+        for tiles in halves:
+            update_gate(t, tiles)
+        for tiles in halves:
+            blend_diff(t, tiles)
+        result = gates.tile([P, ROW_TILES, 2 * P], F32)
+        for half, tiles in enumerate(halves):
+            blend_step(t, tiles)
+            flip_back(banks, t, tiles)
+        for half, tiles in enumerate(halves):
+            add_back(result, banks, PAIRS - 1, half)
+            store(result, PAIRS - 1, tiles)

@@ -44,16 +44,16 @@ def tile_prior_pa_kernel(tc, h, prev_rnn_hidden, W_ih, W_hh, b_ih, b_n, out):
         steps = ctx.enter_context(tc.tile_pool(name="steps", bufs=4))
         psum = ctx.enter_context(tc.psum_pool(name="psum", bufs=8))
 
+        ident = const.tile([P, P], F32)
+        make_identity(nc, ident[:])
         bias_rows = const.tile([P, 2 * P], BF16)
         nc.vector.memset(bias_rows[:], 0.0)
         zero = const.tile([P, 1], F32)
         nc.vector.memset(zero[:], 0.0)
-        nc.scalar.dma_start(out=bias_rows[0:12, :], in_=b_ih.rearrange("(r c) -> r c", c=2 * P))
-        nc.scalar.dma_start(out=bias_rows[12:16, :], in_=b_n.rearrange("(r c) -> r c", c=2 * P))
+        nc.gpsimd.dma_start(out=bias_rows[0:12, :], in_=b_ih.rearrange("(r c) -> r c", c=2 * P))
+        nc.gpsimd.dma_start(out=bias_rows[12:16, :], in_=b_n.rearrange("(r c) -> r c", c=2 * P))
         warm = const.tile([P, 1], F32)
         nc.scalar.activation(out=warm[:], in_=zero[:], func=ACT.Sigmoid)
-        ident = const.tile([P, P], F32)
-        make_identity(nc, ident[:])
 
         inputs = {"ih": h, "hh": prev_rnn_hidden}
         weights = {"ih": W_ih, "hh": W_hh}
@@ -235,13 +235,13 @@ def tile_prior_pa_kernel(tc, h, prev_rnn_hidden, W_ih, W_hh, b_ih, b_n, out):
                 out=gate_tiles["update"][:, rows], in_=sums["z"][:, rows], func=ACT.Sigmoid, bias=bias_of(t, 4 * GATE_Z)
             )
 
-        def blend_diff(t, tiles=ALL):
+        def blend_diff(t, tiles=ALL, engine=nc.vector):
             if tiles.start == 0:
                 gate_tile("diff")
             rows = rows_of(tiles)
             c, e = divmod(t, 2)
             g, u = divmod(c, 2)
-            nc.vector.tensor_tensor(
+            engine.tensor_tensor(
                 out=gate_tiles["diff"][:, rows].rearrange("p (m r) -> p m r", r=P),
                 in0=hp_flipped[:, g, u, e, tiles],
                 in1=gate_tiles["new"][:, rows].rearrange("p (m r) -> p m r", r=P),
@@ -300,16 +300,37 @@ def tile_prior_pa_kernel(tc, h, prev_rnn_hidden, W_ih, W_hh, b_ih, b_n, out):
             regroup_block(pos)
             quantise(0, pos, pos + 1, grouped_pairs[pos // 2][:, pos % 2 * K : (pos % 2 + 1) * K])
         for m in range(ROW_TILES):
-            prepare_rows("hh", m, nc.scalar.copy if m % 2 == 0 else nc.vector.tensor_copy)
+            prepare_rows("hh", m, nc.vector.tensor_copy if m == 1 else nc.scalar.copy)
             if m == 1:
                 transpose_biases()
-        for i, pos in enumerate(HH_BLOCKS):
+        for pos in HH_BLOCKS:
             flip_block(0, pos)
-            regroup_block(pos, nc.scalar.copy if i % 2 == 0 else nc.vector.tensor_copy)
+            regroup_block(pos)
             quantise(0, pos, pos + 1, grouped_pairs[pos // 2][:, pos % 2 * K : (pos % 2 + 1) * K])
         grouped_pairs.clear()
 
-        for t in range(COL_TILES):
+        new_codes()
+        for pos in range(2):
+            flip_block(1, pos)
+            regroup_block(pos)
+            if pos % 2 == 1:
+                quantise_pair(1, pos // 2)
+        sums["r"] = multiply(0, GATE_R, ("ih", "hh"))
+        gate_tile("reset")
+        gate_tile("gated")
+        gate_tile("pre")
+        reset_gate(0)
+        sums["hn"] = multiply(0, GATE_N, ("hh",))
+        gated_sum(0)
+        sums["in"] = multiply(0, GATE_N, ("ih",))
+        before_tanh(0)
+        sums["z"] = multiply(0, GATE_Z, ("ih", "hh"))
+        for pos in range(2, len(BLOCKS)):
+            flip_block(1, pos)
+            regroup_block(pos, nc.vector.tensor_copy if pos in (3, 5) else nc.scalar.copy)
+            if pos % 2 == 1:
+                quantise_pair(1, pos // 2)
+        for t in range(1, COL_TILES):
             c, e = divmod(t, 2)
             more = t + 1 < COL_TILES
             done = t - 1
@@ -332,8 +353,8 @@ def tile_prior_pa_kernel(tc, h, prev_rnn_hidden, W_ih, W_hh, b_ih, b_n, out):
             if done >= 0:
                 gate_tile("new")
                 new_gate(done)
-            if done >= 0 and more:
-                blend_diff(done)
+            if done >= 0:
+                blend_diff(done, engine=nc.vector if more else nc.gpsimd)
             if more:
                 flip_block(t + 1, 1)
                 regroup_block(1)
@@ -365,7 +386,6 @@ def tile_prior_pa_kernel(tc, h, prev_rnn_hidden, W_ih, W_hh, b_ih, b_n, out):
             for tiles in halves:
                 before_tanh(t, tiles)
             if not more:
-                blend_diff(done)
                 blend_step(done)
             if more:
                 quantise_pair(t + 1, 2)

@@ -28,6 +28,7 @@ BLOCK_PAIRS = len(BLOCKS) // 2
 IH_BLOCKS = [pos for pos, (src, gate) in enumerate(BLOCKS) if src == "ih"]
 HH_BLOCKS = [pos for pos, (src, gate) in enumerate(BLOCKS) if src == "hh"]
 BLOCK_WORDS = PASSES * P
+WARM_UP = 4
 FLOPS = 2 * 2 * BATCH * 3 * R * K
 
 
@@ -46,6 +47,13 @@ def tile_prior_pa_kernel(tc, h, prev_rnn_hidden, W_ih, W_hh, b_ih, b_n, out):
 
         ident = const.tile([P, P], F32)
         make_identity(nc, ident[:])
+        ident_bf16 = const.tile([P, P], BF16)
+        make_identity(nc, ident_bf16[:])
+        zeros = const.tile([P, BATCH], BF16)
+        nc.vector.memset(zeros[:], 0.0)
+        idle = psum.tile([P, BATCH], F32, tag="bank")
+        for i in range(WARM_UP):
+            nc.tensor.matmul(idle[:], lhsT=zeros[:, 0:P], rhs=zeros[:], start=True, stop=True)
         bias_rows = const.tile([P, 2 * P], BF16)
         nc.vector.memset(bias_rows[:], 0.0)
         zero = const.tile([P, 1], F32)
@@ -131,9 +139,10 @@ def tile_prior_pa_kernel(tc, h, prev_rnn_hidden, W_ih, W_hh, b_ih, b_n, out):
             bias_bank = psum.tile([P, WORDS], F32, tag="bank")
             for e in range(2):
                 nc.tensor.transpose(bias_bank[:, e * P : (e + 1) * P], bias_parted[:, e, :], ident[:])
-            nc.vector.tensor_copy(
-                out=bias[:], in_=bias_bank[:, 0 : 2 * P].rearrange("p (e r) -> p e r", e=2)[:, :, 0:16]
-            )
+            by_row = bias_bank[:, 0 : 2 * P].rearrange("p (e r) -> p e r", e=2)
+            nc.vector.tensor_copy(out=bias[:], in_=by_row[:, :, 0:16])
+            z_rows = slice(4 * GATE_Z, 4 * GATE_Z + 4)
+            nc.vector.tensor_scalar(out=bias[:, :, z_rows], in0=by_row[:, :, z_rows], scalar1=-1.0, scalar2=None, op0=ALU.mult)
 
         def bias_of(t, row):
             c, e = divmod(t, 2)
@@ -232,7 +241,7 @@ def tile_prior_pa_kernel(tc, h, prev_rnn_hidden, W_ih, W_hh, b_ih, b_n, out):
         def update_gate(t, tiles=ALL):
             rows = rows_of(tiles)
             nc.scalar.activation(
-                out=gate_tiles["update"][:, rows], in_=sums["z"][:, rows], func=ACT.Sigmoid, bias=bias_of(t, 4 * GATE_Z)
+                out=gate_tiles["keep"][:, rows], in_=sums["z"][:, rows], func=ACT.Sigmoid, bias=bias_of(t, 4 * GATE_Z), scale=-1.0
             )
 
         def blend_diff(t, tiles=ALL, engine=nc.vector):
@@ -243,23 +252,18 @@ def tile_prior_pa_kernel(tc, h, prev_rnn_hidden, W_ih, W_hh, b_ih, b_n, out):
             g, u = divmod(c, 2)
             engine.tensor_tensor(
                 out=gate_tiles["diff"][:, rows].rearrange("p (m r) -> p m r", r=P),
-                in0=hp_flipped[:, g, u, e, tiles],
-                in1=gate_tiles["new"][:, rows].rearrange("p (m r) -> p m r", r=P),
+                in0=gate_tiles["new"][:, rows].rearrange("p (m r) -> p m r", r=P),
+                in1=hp_flipped[:, g, u, e, tiles],
                 op=ALU.subtract,
             )
 
-        def blend_step(t, tiles=ALL):
+        def blend_step(t, tiles=ALL, engine=nc.vector):
             if t not in step:
                 step_t = steps.tile([P, BATCH], F32)
                 step[t] = step_t
             rows = rows_of(tiles)
-            nc.vector.scalar_tensor_tensor(
-                out=step[t][:, rows],
-                in0=gate_tiles["update"][:, rows],
-                scalar=-1.0,
-                in1=gate_tiles["diff"][:, rows],
-                op0=ALU.add,
-                op1=ALU.mult,
+            engine.tensor_tensor(
+                out=step[t][:, rows], in0=gate_tiles["keep"][:, rows], in1=gate_tiles["diff"][:, rows], op=ALU.mult
             )
 
         hp_by_tile = act_rows["hh"][:].rearrange("p (m k) -> p m k", m=ROW_TILES)
@@ -287,26 +291,42 @@ def tile_prior_pa_kernel(tc, h, prev_rnn_hidden, W_ih, W_hh, b_ih, b_n, out):
                 op=ALU.add,
             )
 
+        def sum_back(bank, place, c, m):
+            cols = slice(m * K + c * 2 * P, m * K + (c + 1) * 2 * P)
+            nc.tensor.matmul(
+                bank[:, place : place + 2 * P], lhsT=ident_bf16[:], rhs=act_rows["hh"][:, cols], start=True, stop=False
+            )
+
+        def sum_step(bank, place, t, m):
+            woven = bank[:, place : place + 2 * P].rearrange("p (j e) -> p e j", e=2)
+            nc.tensor.matmul(
+                woven[:, t % 2, :],
+                lhsT=step[t][:, m * P : (m + 1) * P],
+                rhs=ident[:],
+                is_transpose=True,
+                start=False,
+                stop=(t % 2 == 1),
+            )
+
         def store(result, c, tiles):
             cols = slice(c * 2 * P, (c + 1) * 2 * P)
             nc.sync.dma_start(out=out_by_tile[:, tiles, cols], in_=result[:, tiles, :])
 
         for m in range(ROW_TILES):
             prepare_rows("ih", m, nc.scalar.copy)
-        part_biases()
         new_codes()
         for pos in IH_BLOCKS:
             flip_block(0, pos)
             regroup_block(pos)
             quantise(0, pos, pos + 1, grouped_pairs[pos // 2][:, pos % 2 * K : (pos % 2 + 1) * K])
+        part_biases()
         for m in range(ROW_TILES):
             prepare_rows("hh", m, nc.vector.tensor_copy if m == 1 else nc.scalar.copy)
-            if m == 1:
-                transpose_biases()
         for pos in HH_BLOCKS:
             flip_block(0, pos)
             regroup_block(pos)
             quantise(0, pos, pos + 1, grouped_pairs[pos // 2][:, pos % 2 * K : (pos % 2 + 1) * K])
+        transpose_biases()
         grouped_pairs.clear()
 
         new_codes()
@@ -330,13 +350,31 @@ def tile_prior_pa_kernel(tc, h, prev_rnn_hidden, W_ih, W_hh, b_ih, b_n, out):
             regroup_block(pos, nc.vector.tensor_copy if pos in (3, 5) else nc.scalar.copy)
             if pos % 2 == 1:
                 quantise_pair(1, pos // 2)
+        back_banks = []
+        back_result = gates.tile([P, ROW_TILES, 2 * P], F32, name="back_result")
+
+        def back_pair(c, half):
+            for m in range(2 * half, 2 * half + 2):
+                back = psum.tile([P, BATCH], F32, tag="bank")
+                back_banks.append(back)
+                sum_back(back, 0, c, m)
+            for m in range(2 * half, 2 * half + 2):
+                sum_step(back_banks[m], 0, 2 * c, m)
+                sum_step(back_banks[m], 0, 2 * c + 1, m)
+
+        def empty_back(c, half):
+            tiles = slice(2 * half, 2 * half + 2)
+            for m in range(2 * half, 2 * half + 2):
+                nc.scalar.copy(out=back_result[:, m, :], in_=back_banks[m][:, 0 : 2 * P])
+            store(back_result, c, tiles)
+
         for t in range(1, COL_TILES):
             c, e = divmod(t, 2)
             more = t + 1 < COL_TILES
             done = t - 1
             if more:
                 new_codes()
-            if e == 1 and c > 0:
+            if e == 1 and c > 0 and more:
                 banks = new_back()
                 flip_back(banks, t - 3)
                 flip_back(banks, t - 2)
@@ -345,7 +383,7 @@ def tile_prior_pa_kernel(tc, h, prev_rnn_hidden, W_ih, W_hh, b_ih, b_n, out):
                 add_back(result, banks, c - 1, 1)
                 store(result, c - 1, ALL)
             if done >= 0:
-                gate_tile("update")
+                gate_tile("keep")
                 update_gate(done)
             if more:
                 flip_block(t + 1, 0)
@@ -359,8 +397,8 @@ def tile_prior_pa_kernel(tc, h, prev_rnn_hidden, W_ih, W_hh, b_ih, b_n, out):
                 flip_block(t + 1, 1)
                 regroup_block(1)
                 quantise_pair(t + 1, 0)
-            if done >= 0 and more:
-                blend_step(done)
+            if done >= 0:
+                blend_step(done, engine=nc.vector if more else nc.gpsimd)
             if more:
                 flip_block(t + 1, 2)
                 regroup_block(2)
@@ -385,27 +423,39 @@ def tile_prior_pa_kernel(tc, h, prev_rnn_hidden, W_ih, W_hh, b_ih, b_n, out):
             sums["in"] = multiply(t, GATE_N, ("ih",))
             for tiles in halves:
                 before_tanh(t, tiles)
-            if not more:
-                blend_step(done)
             if more:
                 quantise_pair(t + 1, 2)
+            if not more:
+                back_pair(c - 1, 0)
+                empty_back(c - 1, 0)
             sums["z"] = multiply(t, GATE_Z, ("ih", "hh"))
 
         t = COL_TILES - 1
-        banks = new_back()
-        flip_back(banks, t - 1)
-        gate_tile("update")
+        c = PAIRS - 2
+        back_pair(c, 1)
+        last_banks = []
+        for m in range(ROW_TILES):
+            back = psum.tile([P, BATCH], F32, tag="bank")
+            last_banks.append(back)
+            sum_back(back, 0, PAIRS - 1, m)
+        for m in range(ROW_TILES):
+            sum_step(last_banks[m], 0, t - 1, m)
+        gate_tile("keep")
         gate_tile("new")
         for tiles in halves:
             new_gate(t, tiles)
         for tiles in halves:
             update_gate(t, tiles)
+        empty_back(c, 1)
         for tiles in halves:
             blend_diff(t, tiles)
         result = gates.tile([P, ROW_TILES, 2 * P], F32)
-        for half, tiles in enumerate(halves):
+        for tiles in halves:
             blend_step(t, tiles)
-            flip_back(banks, t, tiles)
-        for half, tiles in enumerate(halves):
-            add_back(result, banks, PAIRS - 1, half)
+            for m in range(tiles.start, tiles.stop):
+                sum_step(last_banks[m], 0, t, m)
+        for tiles in halves:
+            for m in range(tiles.start, tiles.stop):
+                copy = nc.vector.tensor_copy if m % 2 == 0 else nc.scalar.copy
+                copy(out=result[:, m, :], in_=last_banks[m][:, 0 : 2 * P])
             store(result, PAIRS - 1, tiles)

@@ -291,21 +291,25 @@ def tile_prior_pa_kernel(tc, h, prev_rnn_hidden, W_ih, W_hh, b_ih, b_n, out):
                 op=ALU.add,
             )
 
-        def sum_back(bank, place, c, m):
+        def sum_back(bank, c, m):
             cols = slice(m * K + c * 2 * P, m * K + (c + 1) * 2 * P)
-            nc.tensor.matmul(
-                bank[:, place : place + 2 * P], lhsT=ident_bf16[:], rhs=act_rows["hh"][:, cols], start=True, stop=False
-            )
+            parted = act_rows["hh"][:, cols].rearrange("p (j e) -> p e j", e=2)
+            nc.tensor.matmul(bank[:, 0 : 2 * P], lhsT=ident_bf16[:], rhs=parted, start=True, stop=False)
 
-        def sum_step(bank, place, t, m):
-            woven = bank[:, place : place + 2 * P].rearrange("p (j e) -> p e j", e=2)
+        def sum_step(bank, t, m):
             nc.tensor.matmul(
-                woven[:, t % 2, :],
+                bank[:, t % 2 * P : (t % 2 + 1) * P],
                 lhsT=step[t][:, m * P : (m + 1) * P],
                 rhs=ident[:],
                 is_transpose=True,
                 start=False,
                 stop=(t % 2 == 1),
+            )
+
+        def empty_bank(copy, result, bank, m):
+            copy(
+                out=result[:, m, :].rearrange("p (j e) -> p j e", e=2),
+                in_=bank[:, 0 : 2 * P].rearrange("p (e j) -> p j e", e=2),
             )
 
         def store(result, c, tiles):
@@ -357,15 +361,15 @@ def tile_prior_pa_kernel(tc, h, prev_rnn_hidden, W_ih, W_hh, b_ih, b_n, out):
             for m in range(2 * half, 2 * half + 2):
                 back = psum.tile([P, BATCH], F32, tag="bank")
                 back_banks.append(back)
-                sum_back(back, 0, c, m)
+                sum_back(back, c, m)
             for m in range(2 * half, 2 * half + 2):
-                sum_step(back_banks[m], 0, 2 * c, m)
-                sum_step(back_banks[m], 0, 2 * c + 1, m)
+                sum_step(back_banks[m], 2 * c, m)
+                sum_step(back_banks[m], 2 * c + 1, m)
 
         def empty_back(c, half):
             tiles = slice(2 * half, 2 * half + 2)
             for m in range(2 * half, 2 * half + 2):
-                nc.scalar.copy(out=back_result[:, m, :], in_=back_banks[m][:, 0 : 2 * P])
+                empty_bank(nc.scalar.copy, back_result, back_banks[m], m)
             store(back_result, c, tiles)
 
         for t in range(1, COL_TILES):
@@ -437,9 +441,9 @@ def tile_prior_pa_kernel(tc, h, prev_rnn_hidden, W_ih, W_hh, b_ih, b_n, out):
         for m in range(ROW_TILES):
             back = psum.tile([P, BATCH], F32, tag="bank")
             last_banks.append(back)
-            sum_back(back, 0, PAIRS - 1, m)
+            sum_back(back, PAIRS - 1, m)
         for m in range(ROW_TILES):
-            sum_step(last_banks[m], 0, t - 1, m)
+            sum_step(last_banks[m], t - 1, m)
         gate_tile("keep")
         gate_tile("new")
         for tiles in halves:
@@ -453,9 +457,9 @@ def tile_prior_pa_kernel(tc, h, prev_rnn_hidden, W_ih, W_hh, b_ih, b_n, out):
         for tiles in halves:
             blend_step(t, tiles)
             for m in range(tiles.start, tiles.stop):
-                sum_step(last_banks[m], 0, t, m)
+                sum_step(last_banks[m], t, m)
         for tiles in halves:
             for m in range(tiles.start, tiles.stop):
                 copy = nc.vector.tensor_copy if m % 2 == 0 else nc.scalar.copy
-                copy(out=result[:, m, :], in_=last_banks[m][:, 0 : 2 * P])
+                empty_bank(copy, result, last_banks[m], m)
             store(result, PAIRS - 1, tiles)

@@ -47,8 +47,6 @@ def tile_prior_pa_kernel(tc, h, prev_rnn_hidden, W_ih, W_hh, b_ih, b_n, out):
 
         ident = const.tile([P, P], F32)
         make_identity(nc, ident[:])
-        ident_bf16 = const.tile([P, P], BF16)
-        make_identity(nc, ident_bf16[:])
         zeros = const.tile([P, BATCH], BF16)
         nc.vector.memset(zeros[:], 0.0)
         idle = psum.tile([P, BATCH], F32, tag="bank")
@@ -60,6 +58,8 @@ def tile_prior_pa_kernel(tc, h, prev_rnn_hidden, W_ih, W_hh, b_ih, b_n, out):
         nc.vector.memset(zero[:], 0.0)
         nc.gpsimd.dma_start(out=bias_rows[0:12, :], in_=b_ih.rearrange("(r c) -> r c", c=2 * P))
         nc.gpsimd.dma_start(out=bias_rows[12:16, :], in_=b_n.rearrange("(r c) -> r c", c=2 * P))
+        ident_bf16 = const.tile([P, P], BF16)
+        make_identity(nc, ident_bf16[:])
         warm = const.tile([P, 1], F32)
         nc.scalar.activation(out=warm[:], in_=zero[:], func=ACT.Sigmoid)
 
@@ -176,8 +176,10 @@ def tile_prior_pa_kernel(tc, h, prev_rnn_hidden, W_ih, W_hh, b_ih, b_n, out):
         def quantise_pair(t, q):
             quantise(t, 2 * q, 2 * q + 2, grouped_pairs.pop(q)[:])
 
-        def multiply(t, gate, sources):
-            total = psum.tile([P, BATCH], F32, tag="bank")
+        def multiply(t, gate, sources, total=None, last=True):
+            first_pass = total is None
+            if first_pass:
+                total = psum.tile([P, BATCH], F32, tag="bank")
             passes = [(src, g) for src in sources for g in range(PASSES)]
             for i, (src, g) in enumerate(passes):
                 first = BLOCKS.index((src, gate)) * BLOCK_WORDS + g * P
@@ -189,8 +191,8 @@ def tile_prior_pa_kernel(tc, h, prev_rnn_hidden, W_ih, W_hh, b_ih, b_n, out):
                     lhsT_scale=w_scales[t][:, w_cols],
                     rhs=act_codes[src][:, a_cols].bitcast(FP8X4),
                     rhs_scale=act_scales[src][:, a_cols],
-                    start=(i == 0),
-                    stop=(i == len(passes) - 1),
+                    start=(first_pass and i == 0),
+                    stop=(last and i == len(passes) - 1),
                 )
             return total
 
@@ -349,11 +351,20 @@ def tile_prior_pa_kernel(tc, h, prev_rnn_hidden, W_ih, W_hh, b_ih, b_n, out):
         sums["in"] = multiply(0, GATE_N, ("ih",))
         before_tanh(0)
         sums["z"] = multiply(0, GATE_Z, ("ih", "hh"))
-        for pos in range(2, len(BLOCKS)):
+        gate_tile("keep")
+        gate_tile("new")
+        for i, pos in enumerate(range(2, len(BLOCKS))):
             flip_block(1, pos)
             regroup_block(pos, nc.vector.tensor_copy if pos in (3, 5) else nc.scalar.copy)
+            if i == 0:
+                update_gate(0)
+            if i == 1:
+                new_gate(0)
+            if i == 2:
+                blend_diff(0)
             if pos % 2 == 1:
                 quantise_pair(1, pos // 2)
+        blend_step(0)
         back_banks = []
         back_result = gates.tile([P, ROW_TILES, 2 * P], F32, name="back_result")
 
@@ -386,23 +397,23 @@ def tile_prior_pa_kernel(tc, h, prev_rnn_hidden, W_ih, W_hh, b_ih, b_n, out):
                 add_back(result, banks, c - 1, 0)
                 add_back(result, banks, c - 1, 1)
                 store(result, c - 1, ALL)
-            if done >= 0:
+            if done > 0:
                 gate_tile("keep")
                 update_gate(done)
             if more:
                 flip_block(t + 1, 0)
                 regroup_block(0)
-            if done >= 0:
+            if done > 0:
                 gate_tile("new")
                 new_gate(done)
-            if done >= 0:
-                blend_diff(done, engine=nc.vector if more else nc.gpsimd)
+            if done > 0:
+                blend_diff(done)
             if more:
                 flip_block(t + 1, 1)
                 regroup_block(1)
                 quantise_pair(t + 1, 0)
-            if done >= 0:
-                blend_step(done, engine=nc.vector if more else nc.gpsimd)
+            if done > 0 and more:
+                blend_step(done)
             if more:
                 flip_block(t + 1, 2)
                 regroup_block(2)
@@ -430,6 +441,7 @@ def tile_prior_pa_kernel(tc, h, prev_rnn_hidden, W_ih, W_hh, b_ih, b_n, out):
             if more:
                 quantise_pair(t + 1, 2)
             if not more:
+                blend_step(done)
                 back_pair(c - 1, 0)
                 empty_back(c - 1, 0)
             sums["z"] = multiply(t, GATE_Z, ("ih", "hh"))
@@ -437,13 +449,8 @@ def tile_prior_pa_kernel(tc, h, prev_rnn_hidden, W_ih, W_hh, b_ih, b_n, out):
         t = COL_TILES - 1
         c = PAIRS - 2
         back_pair(c, 1)
-        last_banks = []
-        for m in range(ROW_TILES):
-            back = psum.tile([P, BATCH], F32, tag="bank")
-            last_banks.append(back)
-            sum_back(back, PAIRS - 1, m)
-        for m in range(ROW_TILES):
-            sum_step(last_banks[m], t - 1, m)
+        banks = new_back()
+        flip_back(banks, t - 1)
         gate_tile("keep")
         gate_tile("new")
         for tiles in halves:
@@ -456,10 +463,7 @@ def tile_prior_pa_kernel(tc, h, prev_rnn_hidden, W_ih, W_hh, b_ih, b_n, out):
         result = gates.tile([P, ROW_TILES, 2 * P], F32)
         for tiles in halves:
             blend_step(t, tiles)
-            for m in range(tiles.start, tiles.stop):
-                sum_step(last_banks[m], t, m)
-        for tiles in halves:
-            for m in range(tiles.start, tiles.stop):
-                copy = nc.vector.tensor_copy if m % 2 == 0 else nc.scalar.copy
-                empty_bank(copy, result, last_banks[m], m)
+            flip_back(banks, t, tiles)
+        for half, tiles in enumerate(halves):
+            add_back(result, banks, PAIRS - 1, half)
             store(result, PAIRS - 1, tiles)

@@ -71,11 +71,12 @@ def tile_prior_pa_kernel(tc, h, prev_rnn_hidden, W_ih, W_hh, b_ih, b_n, out):
             rows = rows_pool.tile([P, len(BLOCKS) * K], BF16, tag="w_rows", name="w_rows")
             w_rows.append(rows)
 
-        def load_activations(src):
-            rows = acts.tile([P, ROW_TILES * K], BF16, name="act_rows_" + src)
+        def load_activations(src, splits):
+            rows = acts.tile([P, ROW_TILES, K], BF16, name="act_rows_" + src)
             act_rows[src] = rows
-            for m in range(ROW_TILES):
-                nc.sync.dma_start(out=rows[:, m * K : (m + 1) * K], in_=inputs[src][m * P : (m + 1) * P, :])
+            by_tile = inputs[src].rearrange("(p m) k -> p m k", m=ROW_TILES)
+            for first, last in splits:
+                nc.sync.dma_start(out=rows[:, first:last, :], in_=by_tile[:, first:last, :])
 
         def load_weight_blocks(t, positions):
             c, e = divmod(t, 2)
@@ -85,9 +86,9 @@ def tile_prior_pa_kernel(tc, h, prev_rnn_hidden, W_ih, W_hh, b_ih, b_n, out):
                 both = weights[src][first : first + 2 * P, :].rearrange("(p e) k -> p e k", e=2)
                 nc.sync.dma_start(out=w_rows[t][:, pos * K : (pos + 1) * K], in_=both[:, e, :])
 
-        load_activations("ih")
+        load_activations("ih", [(0, 2), (2, 4)])
         load_weight_blocks(0, IH_BLOCKS)
-        load_activations("hh")
+        load_activations("hh", [(0, 2), (2, 4)])
         load_weight_blocks(0, HH_BLOCKS)
         for t in range(1, COL_TILES):
             load_weight_blocks(t, range(len(BLOCKS)))
@@ -117,7 +118,7 @@ def tile_prior_pa_kernel(tc, h, prev_rnn_hidden, W_ih, W_hh, b_ih, b_n, out):
             act_scales[src] = scales
 
         def prepare_rows(src, m, copy):
-            flipped = flip(act_rows[src][:].bitcast(F32)[:, m * WORDS : (m + 1) * WORDS])
+            flipped = flip(act_rows[src][:, m, :].bitcast(F32))
             grouped = act_grouped[src][:, m * K : (m + 1) * K]
             regroup(copy, grouped, flipped)
             for g in range(PASSES):
@@ -268,8 +269,8 @@ def tile_prior_pa_kernel(tc, h, prev_rnn_hidden, W_ih, W_hh, b_ih, b_n, out):
                 out=step[t][:, rows], in0=gate_tiles["keep"][:, rows], in1=gate_tiles["diff"][:, rows], op=ALU.mult
             )
 
-        hp_by_tile = act_rows["hh"][:].rearrange("p (m k) -> p m k", m=ROW_TILES)
-        out_by_tile = out.rearrange("(m p) j -> p m j", p=P)
+        hp_by_tile = act_rows["hh"]
+        out_by_tile = out.rearrange("(p m) j -> p m j", m=ROW_TILES)
 
         def new_back():
             banks = []
@@ -294,8 +295,8 @@ def tile_prior_pa_kernel(tc, h, prev_rnn_hidden, W_ih, W_hh, b_ih, b_n, out):
             )
 
         def sum_back(bank, c, m):
-            cols = slice(m * K + c * 2 * P, m * K + (c + 1) * 2 * P)
-            parted = act_rows["hh"][:, cols].rearrange("p (j e) -> p e j", e=2)
+            cols = slice(c * 2 * P, (c + 1) * 2 * P)
+            parted = act_rows["hh"][:, m, cols].rearrange("p (j e) -> p e j", e=2)
             nc.tensor.matmul(bank[:, 0 : 2 * P], lhsT=ident_bf16[:], rhs=parted, start=True, stop=False)
 
         def sum_step(bank, t, m):

@@ -28,6 +28,8 @@ BLOCK_PAIRS = len(BLOCKS) // 2
 IH_BLOCKS = [pos for pos, (src, gate) in enumerate(BLOCKS) if src == "ih"]
 HH_BLOCKS = [pos for pos, (src, gate) in enumerate(BLOCKS) if src == "hh"]
 BLOCK_WORDS = PASSES * P
+BANKS = 8
+DVE_MOD = 2
 WARM_UP = 4
 FLOPS = 2 * 2 * BATCH * 3 * R * K
 
@@ -43,13 +45,23 @@ def tile_prior_pa_kernel(tc, h, prev_rnn_hidden, W_ih, W_hh, b_ih, b_n, out):
         quantised = ctx.enter_context(tc.tile_pool(name="quantised", bufs=2))
         gates = ctx.enter_context(tc.tile_pool(name="gates", bufs=2))
         steps = ctx.enter_context(tc.tile_pool(name="steps", bufs=4))
-        psum = ctx.enter_context(tc.psum_pool(name="psum", bufs=8))
+        psum = ctx.enter_context(tc.psum_pool(name="psum", bufs=1))
+        ring = {"next": 0}
+        held = set()
+
+        def new_bank():
+            while ring["next"] in held:
+                ring["next"] = (ring["next"] + 1) % BANKS
+            number = ring["next"]
+            ring["next"] = (number + 1) % BANKS
+            bank = psum.tile([P, BATCH], F32, tag="bank%d" % number, name="bank%d" % number)
+            return bank, number
 
         ident = const.tile([P, P], F32)
         make_identity(nc, ident[:])
         zeros = const.tile([P, BATCH], BF16)
         nc.vector.memset(zeros[:], 0.0)
-        idle = psum.tile([P, BATCH], F32, tag="bank")
+        idle, number = new_bank()
         for i in range(WARM_UP):
             nc.tensor.matmul(idle[:], lhsT=zeros[:, 0:P], rhs=zeros[:], start=True, stop=True)
         bias_rows = const.tile([P, 2 * P], BF16)
@@ -94,7 +106,7 @@ def tile_prior_pa_kernel(tc, h, prev_rnn_hidden, W_ih, W_hh, b_ih, b_n, out):
             load_weight_blocks(t, range(len(BLOCKS)))
 
         def flip(words):
-            flipped = psum.tile([P, WORDS], F32, tag="bank")
+            flipped, number = new_bank()
             for c in range(CHUNKS):
                 cols = slice(c * P, (c + 1) * P)
                 nc.tensor.transpose(flipped[:, cols], words[:, cols], ident[:])
@@ -117,10 +129,16 @@ def tile_prior_pa_kernel(tc, h, prev_rnn_hidden, W_ih, W_hh, b_ih, b_n, out):
             act_codes[src] = codes
             act_scales[src] = scales
 
-        def prepare_rows(src, m, copy):
-            flipped = flip(act_rows[src][:, m, :].bitcast(F32))
+        flipped_rows = {}
+
+        def flip_rows(src, m):
+            flipped_rows[src, m] = flip(act_rows[src][:, m, :].bitcast(F32))
+
+        def regroup_rows(src, m, copy):
+            regroup(copy, act_grouped[src][:, m * K : (m + 1) * K], flipped_rows.pop((src, m)))
+
+        def quantise_rows(src, m):
             grouped = act_grouped[src][:, m * K : (m + 1) * K]
-            regroup(copy, grouped, flipped)
             for g in range(PASSES):
                 cols = slice(g * BATCH + m * P, g * BATCH + (m + 1) * P)
                 nc.vector.quantize_mx(
@@ -137,7 +155,7 @@ def tile_prior_pa_kernel(tc, h, prev_rnn_hidden, W_ih, W_hh, b_ih, b_n, out):
             nc.vector.tensor_copy(out=bias_parted[:], in_=bias_rows[:].rearrange("r (p e) -> r e p", e=2))
 
         def transpose_biases():
-            bias_bank = psum.tile([P, WORDS], F32, tag="bank")
+            bias_bank, number = new_bank()
             for e in range(2):
                 nc.tensor.transpose(bias_bank[:, e * P : (e + 1) * P], bias_parted[:, e, :], ident[:])
             by_row = bias_bank[:, 0 : 2 * P].rearrange("p (e r) -> p e r", e=2)
@@ -177,10 +195,12 @@ def tile_prior_pa_kernel(tc, h, prev_rnn_hidden, W_ih, W_hh, b_ih, b_n, out):
         def quantise_pair(t, q):
             quantise(t, 2 * q, 2 * q + 2, grouped_pairs.pop(q)[:])
 
-        def multiply(t, gate, sources, total=None, last=True):
+        def multiply(t, gate, sources, total=None, last=True, hold=False):
             first_pass = total is None
             if first_pass:
-                total = psum.tile([P, BATCH], F32, tag="bank")
+                total, number = new_bank()
+                if hold:
+                    held.add(number)
             passes = [(src, g) for src in sources for g in range(PASSES)]
             for i, (src, g) in enumerate(passes):
                 first = BLOCKS.index((src, gate)) * BLOCK_WORDS + g * P
@@ -275,7 +295,7 @@ def tile_prior_pa_kernel(tc, h, prev_rnn_hidden, W_ih, W_hh, b_ih, b_n, out):
         def new_back():
             banks = []
             for half in range(2):
-                back = psum.tile([P, BATCH], F32, tag="bank")
+                back, number = new_bank()
                 banks.append(back)
             return banks
 
@@ -319,20 +339,56 @@ def tile_prior_pa_kernel(tc, h, prev_rnn_hidden, W_ih, W_hh, b_ih, b_n, out):
             cols = slice(c * 2 * P, (c + 1) * 2 * P)
             nc.sync.dma_start(out=out_by_tile[:, tiles, cols], in_=result[:, tiles, :])
 
-        for m in range(ROW_TILES):
-            prepare_rows("ih", m, nc.scalar.copy)
+        def half_of_pair(pos):
+            return grouped_pairs[pos // 2][:, pos % 2 * K : (pos % 2 + 1) * K]
+
+        late = []
+
+        def head_step(number, flip_it, regroup_it, quantise_it):
+            flip_it()
+            regroup_it(nc.vector.tensor_copy if number % 3 == DVE_MOD else nc.scalar.copy)
+            if late:
+                late.pop()()
+            late.append(quantise_it)
+
+        def head_rows(number, src, m):
+            head_step(
+                number,
+                lambda: flip_rows(src, m),
+                lambda copy: regroup_rows(src, m, copy),
+                lambda: quantise_rows(src, m),
+            )
+
+        def head_block(number, pos):
+            head_step(
+                number,
+                lambda: flip_block(0, pos),
+                lambda copy: regroup_block(pos, copy),
+                lambda: quantise(0, pos, pos + 1, half_of_pair(pos)),
+            )
+
         new_codes()
-        for pos in IH_BLOCKS:
-            flip_block(0, pos)
-            regroup_block(pos)
-            quantise(0, pos, pos + 1, grouped_pairs[pos // 2][:, pos % 2 * K : (pos % 2 + 1) * K])
-        part_biases()
+        n = 0
         for m in range(ROW_TILES):
-            prepare_rows("hh", m, nc.vector.tensor_copy if m == 1 else nc.scalar.copy)
+            head_rows(n, "ih", m)
+            n += 1
+        for pos in IH_BLOCKS:
+            head_block(n, pos)
+            n += 1
+        part_biases()
+        for m in range(2):
+            head_rows(n, "hh", m)
+            n += 1
+        sums["r"] = multiply(0, GATE_R, ("ih",), last=False, hold=True)
+        sums["in"] = multiply(0, GATE_N, ("ih",), hold=True)
+        sums["z"] = multiply(0, GATE_Z, ("ih",), last=False, hold=True)
+        for m in range(2, ROW_TILES):
+            head_rows(n, "hh", m)
+            n += 1
         for pos in HH_BLOCKS:
-            flip_block(0, pos)
-            regroup_block(pos)
-            quantise(0, pos, pos + 1, grouped_pairs[pos // 2][:, pos % 2 * K : (pos % 2 + 1) * K])
+            head_block(n, pos)
+            n += 1
+        late.pop()()
         transpose_biases()
         grouped_pairs.clear()
 
@@ -342,16 +398,15 @@ def tile_prior_pa_kernel(tc, h, prev_rnn_hidden, W_ih, W_hh, b_ih, b_n, out):
             regroup_block(pos)
             if pos % 2 == 1:
                 quantise_pair(1, pos // 2)
-        sums["r"] = multiply(0, GATE_R, ("ih", "hh"))
+        multiply(0, GATE_R, ("hh",), total=sums["r"])
         gate_tile("reset")
         gate_tile("gated")
         gate_tile("pre")
         reset_gate(0)
-        sums["hn"] = multiply(0, GATE_N, ("hh",))
+        sums["hn"] = multiply(0, GATE_N, ("hh",), hold=True)
         gated_sum(0)
-        sums["in"] = multiply(0, GATE_N, ("ih",))
         before_tanh(0)
-        sums["z"] = multiply(0, GATE_Z, ("ih", "hh"))
+        multiply(0, GATE_Z, ("hh",), total=sums["z"])
         gate_tile("keep")
         gate_tile("new")
         for i, pos in enumerate(range(2, len(BLOCKS))):
@@ -365,13 +420,14 @@ def tile_prior_pa_kernel(tc, h, prev_rnn_hidden, W_ih, W_hh, b_ih, b_n, out):
                 blend_diff(0)
             if pos % 2 == 1:
                 quantise_pair(1, pos // 2)
+        held.clear()
         blend_step(0)
         back_banks = []
         back_result = gates.tile([P, ROW_TILES, 2 * P], F32, name="back_result")
 
         def back_pair(c, half):
             for m in range(2 * half, 2 * half + 2):
-                back = psum.tile([P, BATCH], F32, tag="bank")
+                back, number = new_bank()
                 back_banks.append(back)
                 sum_back(back, c, m)
             for m in range(2 * half, 2 * half + 2):

@@ -29,7 +29,6 @@ IH_BLOCKS = [pos for pos, (src, gate) in enumerate(BLOCKS) if src == "ih"]
 HH_BLOCKS = [pos for pos, (src, gate) in enumerate(BLOCKS) if src == "hh"]
 BLOCK_WORDS = PASSES * P
 BANKS = 8
-DVE_MOD = 2
 WARM_UP = 4
 FLOPS = 2 * 2 * BATCH * 3 * R * K
 
@@ -129,16 +128,10 @@ def tile_prior_pa_kernel(tc, h, prev_rnn_hidden, W_ih, W_hh, b_ih, b_n, out):
             act_codes[src] = codes
             act_scales[src] = scales
 
-        flipped_rows = {}
-
-        def flip_rows(src, m):
-            flipped_rows[src, m] = flip(act_rows[src][:, m, :].bitcast(F32))
-
-        def regroup_rows(src, m, copy):
-            regroup(copy, act_grouped[src][:, m * K : (m + 1) * K], flipped_rows.pop((src, m)))
-
-        def quantise_rows(src, m):
+        def prepare_rows(src, m, copy):
+            flipped = flip(act_rows[src][:, m, :].bitcast(F32))
             grouped = act_grouped[src][:, m * K : (m + 1) * K]
+            regroup(copy, grouped, flipped)
             for g in range(PASSES):
                 cols = slice(g * BATCH + m * P, g * BATCH + (m + 1) * P)
                 nc.vector.quantize_mx(
@@ -166,6 +159,8 @@ def tile_prior_pa_kernel(tc, h, prev_rnn_hidden, W_ih, W_hh, b_ih, b_n, out):
         def bias_of(t, row):
             c, e = divmod(t, 2)
             return bias[:, e, row + c : row + c + 1]
+
+        ALL = slice(0, ROW_TILES)
 
         w_codes = []
         w_scales = []
@@ -195,7 +190,7 @@ def tile_prior_pa_kernel(tc, h, prev_rnn_hidden, W_ih, W_hh, b_ih, b_n, out):
         def quantise_pair(t, q):
             quantise(t, 2 * q, 2 * q + 2, grouped_pairs.pop(q)[:])
 
-        def multiply(t, gate, sources, total=None, last=True, hold=False):
+        def multiply(t, gate, sources, total=None, last=True, hold=False, tiles=ALL, opens=False):
             first_pass = total is None
             if first_pass:
                 total, number = new_bank()
@@ -205,14 +200,14 @@ def tile_prior_pa_kernel(tc, h, prev_rnn_hidden, W_ih, W_hh, b_ih, b_n, out):
             for i, (src, g) in enumerate(passes):
                 first = BLOCKS.index((src, gate)) * BLOCK_WORDS + g * P
                 w_cols = slice(first, first + P)
-                a_cols = slice(g * BATCH, (g + 1) * BATCH)
+                a_cols = slice(g * BATCH + tiles.start * P, g * BATCH + tiles.stop * P)
                 nc.tensor.matmul_mx(
-                    out=total[:],
+                    out=total[:, tiles.start * P : tiles.stop * P],
                     lhsT=w_codes[t][:, w_cols].bitcast(FP8X4),
                     lhsT_scale=w_scales[t][:, w_cols],
                     rhs=act_codes[src][:, a_cols].bitcast(FP8X4),
                     rhs_scale=act_scales[src][:, a_cols],
-                    start=(first_pass and i == 0),
+                    start=((first_pass or opens) and i == 0),
                     stop=(last and i == len(passes) - 1),
                 )
             return total
@@ -223,7 +218,6 @@ def tile_prior_pa_kernel(tc, h, prev_rnn_hidden, W_ih, W_hh, b_ih, b_n, out):
         sums = {}
         gate_tiles = {}
         step = {}
-        ALL = slice(0, ROW_TILES)
 
         def gate_tile(name):
             made = gates.tile([P, BATCH], F32, tag=name, name=name)
@@ -339,56 +333,25 @@ def tile_prior_pa_kernel(tc, h, prev_rnn_hidden, W_ih, W_hh, b_ih, b_n, out):
             cols = slice(c * 2 * P, (c + 1) * 2 * P)
             nc.sync.dma_start(out=out_by_tile[:, tiles, cols], in_=result[:, tiles, :])
 
-        def half_of_pair(pos):
-            return grouped_pairs[pos // 2][:, pos % 2 * K : (pos % 2 + 1) * K]
-
-        late = []
-
-        def head_step(number, flip_it, regroup_it, quantise_it):
-            flip_it()
-            regroup_it(nc.vector.tensor_copy if number % 3 == DVE_MOD else nc.scalar.copy)
-            if late:
-                late.pop()()
-            late.append(quantise_it)
-
-        def head_rows(number, src, m):
-            head_step(
-                number,
-                lambda: flip_rows(src, m),
-                lambda copy: regroup_rows(src, m, copy),
-                lambda: quantise_rows(src, m),
-            )
-
-        def head_block(number, pos):
-            head_step(
-                number,
-                lambda: flip_block(0, pos),
-                lambda copy: regroup_block(pos, copy),
-                lambda: quantise(0, pos, pos + 1, half_of_pair(pos)),
-            )
-
-        new_codes()
-        n = 0
         for m in range(ROW_TILES):
-            head_rows(n, "ih", m)
-            n += 1
+            prepare_rows("ih", m, nc.scalar.copy)
+        new_codes()
         for pos in IH_BLOCKS:
-            head_block(n, pos)
-            n += 1
+            flip_block(0, pos)
+            regroup_block(pos)
+            quantise(0, pos, pos + 1, grouped_pairs[pos // 2][:, pos % 2 * K : (pos % 2 + 1) * K])
         part_biases()
         for m in range(2):
-            head_rows(n, "hh", m)
-            n += 1
+            prepare_rows("hh", m, nc.vector.tensor_copy if m == 1 else nc.scalar.copy)
         sums["r"] = multiply(0, GATE_R, ("ih",), last=False, hold=True)
         sums["in"] = multiply(0, GATE_N, ("ih",), hold=True)
         sums["z"] = multiply(0, GATE_Z, ("ih",), last=False, hold=True)
         for m in range(2, ROW_TILES):
-            head_rows(n, "hh", m)
-            n += 1
+            prepare_rows("hh", m, nc.scalar.copy)
         for pos in HH_BLOCKS:
-            head_block(n, pos)
-            n += 1
-        late.pop()()
+            flip_block(0, pos)
+            regroup_block(pos)
+            quantise(0, pos, pos + 1, grouped_pairs[pos // 2][:, pos % 2 * K : (pos % 2 + 1) * K])
         transpose_biases()
         grouped_pairs.clear()
 
@@ -454,6 +417,14 @@ def tile_prior_pa_kernel(tc, h, prev_rnn_hidden, W_ih, W_hh, b_ih, b_n, out):
                 add_back(result, banks, c - 1, 0)
                 add_back(result, banks, c - 1, 1)
                 store(result, c - 1, ALL)
+            if not more:
+                banks = new_back()
+                flip_back(banks, t - 3)
+                flip_back(banks, t - 2)
+                result = gates.tile([P, ROW_TILES, 2 * P], F32)
+                add_back(result, banks, PAIRS - 2, 0)
+                add_back(result, banks, PAIRS - 2, 1)
+                store(result, PAIRS - 2, ALL)
             if done > 0:
                 gate_tile("keep")
                 update_gate(done)
@@ -464,7 +435,7 @@ def tile_prior_pa_kernel(tc, h, prev_rnn_hidden, W_ih, W_hh, b_ih, b_n, out):
                 gate_tile("new")
                 new_gate(done)
             if done > 0:
-                blend_diff(done)
+                blend_diff(done, engine=nc.vector if more else nc.gpsimd)
             if more:
                 flip_block(t + 1, 1)
                 regroup_block(1)
@@ -498,29 +469,30 @@ def tile_prior_pa_kernel(tc, h, prev_rnn_hidden, W_ih, W_hh, b_ih, b_n, out):
             if more:
                 quantise_pair(t + 1, 2)
             if not more:
-                blend_step(done)
-                back_pair(c - 1, 0)
-                empty_back(c - 1, 0)
+                blend_step(done, engine=nc.gpsimd)
+                gate_tile("new")
+                new_gate(t, halves[0])
+                new_gate(t, halves[1])
+                blend_diff(t, halves[0])
+                blend_diff(t, halves[1])
             sums["z"] = multiply(t, GATE_Z, ("ih", "hh"))
 
         t = COL_TILES - 1
-        c = PAIRS - 2
-        back_pair(c, 1)
-        banks = new_back()
-        flip_back(banks, t - 1)
+        c = PAIRS - 1
+        result = gates.tile([P, ROW_TILES, 2 * P], F32)
         gate_tile("keep")
-        gate_tile("new")
-        for tiles in halves:
-            new_gate(t, tiles)
         for tiles in halves:
             update_gate(t, tiles)
-        empty_back(c, 1)
-        for tiles in halves:
-            blend_diff(t, tiles)
-        result = gates.tile([P, ROW_TILES, 2 * P], F32)
-        for tiles in halves:
-            blend_step(t, tiles)
-            flip_back(banks, t, tiles)
+        for m in range(ROW_TILES):
+            back, number = new_bank()
+            back_banks.append(back)
+            sum_back(back, c, m)
+        for m in range(ROW_TILES):
+            sum_step(back_banks[m], t - 1, m)
         for half, tiles in enumerate(halves):
-            add_back(result, banks, PAIRS - 1, half)
-            store(result, PAIRS - 1, tiles)
+            blend_step(t, tiles)
+            for m in range(tiles.start, tiles.stop):
+                sum_step(back_banks[m], t, m)
+        for m in range(ROW_TILES):
+            empty_bank(nc.scalar.copy if m % 2 == 0 else nc.vector.tensor_copy, result, back_banks[m], m)
+            store(result, c, slice(m, m + 1))

@@ -60,9 +60,13 @@ def tile_prior_pa_kernel(tc, h, prev_rnn_hidden, W_ih, W_hh, b_ih, b_n, out):
         make_identity(nc, ident[:])
         zeros = const.tile([P, BATCH], BF16)
         nc.vector.memset(zeros[:], 0.0)
-        idle, number = new_bank()
-        for i in range(WARM_UP):
-            nc.tensor.matmul(idle[:], lhsT=zeros[:, 0:P], rhs=zeros[:], start=True, stop=True)
+
+        def keep_warm(times):
+            idle, number = new_bank()
+            for i in range(times):
+                nc.tensor.matmul(idle[:], lhsT=zeros[:, 0:P], rhs=zeros[:], start=True, stop=True)
+
+        keep_warm(WARM_UP)
         bias_rows = const.tile([P, 2 * P], BF16)
         nc.vector.memset(bias_rows[:], 0.0)
         zero = const.tile([P, 1], F32)
@@ -340,6 +344,7 @@ def tile_prior_pa_kernel(tc, h, prev_rnn_hidden, W_ih, W_hh, b_ih, b_n, out):
             flip_block(0, pos)
             regroup_block(pos)
             quantise(0, pos, pos + 1, grouped_pairs[pos // 2][:, pos % 2 * K : (pos % 2 + 1) * K])
+        keep_warm(2)
         part_biases()
         for m in range(2):
             prepare_rows("hh", m, nc.vector.tensor_copy if m == 1 else nc.scalar.copy)

from contextlib import ExitStack

import concourse.mybir as mybir
from concourse.masks import make_identity

F32 = mybir.dt.float32
BF16 = mybir.dt.bfloat16
U32 = mybir.dt.uint32
U8 = mybir.dt.uint8
FP8X4 = mybir.dt.float8_e4m3fn_x4
ACT = mybir.ActivationFunctionType
ALU = mybir.AluOpType

P = 128
BATCH = 512
K = 1024
R = 1024
K_PASS = 4 * P
PASSES = K // K_PASS
WORDS = K // 2
CHUNKS = WORDS // P
ROW_TILES = BATCH // P
COL_TILES = R // P
PAIRS = COL_TILES // 2
GATE_R, GATE_Z, GATE_N = 0, 1, 2
BLOCKS = [("ih", GATE_R), ("hh", GATE_R), ("hh", GATE_N), ("ih", GATE_N), ("ih", GATE_Z), ("hh", GATE_Z)]
BLOCK_PAIRS = len(BLOCKS) // 2
IH_BLOCKS = [pos for pos, (src, gate) in enumerate(BLOCKS) if src == "ih"]
HH_BLOCKS = [pos for pos, (src, gate) in enumerate(BLOCKS) if src == "hh"]
BLOCK_WORDS = PASSES * P
BANKS = 8
WARM_UP = 4
FLOPS = 2 * 2 * BATCH * 3 * R * K


def tile_prior_pa_kernel(tc, h, prev_rnn_hidden, W_ih, W_hh, b_ih, b_n, out):
    nc = tc.nc
    with ExitStack() as ctx:
        ctx.enter_context(tc.manual_schedule())
        const = ctx.enter_context(tc.tile_pool(name="const", bufs=1))
        acts = ctx.enter_context(tc.tile_pool(name="acts", bufs=1))
        rows_pool = ctx.enter_context(tc.tile_pool(name="rows", bufs=COL_TILES))
        stage = ctx.enter_context(tc.tile_pool(name="stage", bufs=4))
        quantised = ctx.enter_context(tc.tile_pool(name="quantised", bufs=2))
        gates = ctx.enter_context(tc.tile_pool(name="gates", bufs=2))
        steps = ctx.enter_context(tc.tile_pool(name="steps", bufs=4))
        psum = ctx.enter_context(tc.psum_pool(name="psum", bufs=1))
        ring = {"next": 0}
        held = set()

        def new_bank():
            while ring["next"] in held:
                ring["next"] = (ring["next"] + 1) % BANKS
            number = ring["next"]
            ring["next"] = (number + 1) % BANKS
            bank = psum.tile([P, BATCH], F32, tag="bank%d" % number, name="bank%d" % number)
            return bank, number

        ident = const.tile([P, P], F32)
        make_identity(nc, ident[:])
        zeros = const.tile([P, BATCH], BF16)
        nc.vector.memset(zeros[:], 0.0)

        def keep_warm(times):
            idle, number = new_bank()
            for i in range(times):
                nc.tensor.matmul(idle[:], lhsT=zeros[:, 0:P], rhs=zeros[:], start=True, stop=True)

        keep_warm(WARM_UP)
        bias_rows = const.tile([P, 2 * P], BF16)
        nc.vector.memset(bias_rows[:], 0.0)
        zero = const.tile([P, 1], F32)
        nc.vector.memset(zero[:], 0.0)
        nc.gpsimd.dma_start(out=bias_rows[0:12, :], in_=b_ih.rearrange("(r c) -> r c", c=2 * P))
        nc.gpsimd.dma_start(out=bias_rows[12:16, :], in_=b_n.rearrange("(r c) -> r c", c=2 * P))
        ident_bf16 = const.tile([P, P], BF16)
        make_identity(nc, ident_bf16[:])
        warm = const.tile([P, 1], F32)
        nc.scalar.activation(out=warm[:], in_=zero[:], func=ACT.Sigmoid)

        inputs = {"ih": h, "hh": prev_rnn_hidden}
        weights = {"ih": W_ih, "hh": W_hh}
        act_rows = {}
        w_rows = []
        for t in range(COL_TILES):
            rows = rows_pool.tile([P, len(BLOCKS) * K], BF16, tag="w_rows", name="w_rows")
            w_rows.append(rows)

        def load_activations(src, splits):
            rows = acts.tile([P, ROW_TILES, K], BF16, name="act_rows_" + src)
            act_rows[src] = rows
            by_tile = inputs[src].rearrange("(p m) k -> p m k", m=ROW_TILES)
            for first, last in splits:
                nc.sync.dma_start(out=rows[:, first:last, :], in_=by_tile[:, first:last, :])

        def load_weight_blocks(t, positions):
            c, e = divmod(t, 2)
            for pos in positions:
                src, gate = BLOCKS[pos]
                first = gate * R + c * 2 * P
                both = weights[src][first : first + 2 * P, :].rearrange("(p e) k -> p e k", e=2)
                nc.sync.dma_start(out=w_rows[t][:, pos * K : (pos + 1) * K], in_=both[:, e, :])

        load_activations("ih", [(0, 2), (2, 4)])
        load_weight_blocks(0, IH_BLOCKS)
        load_activations("hh", [(0, 2), (2, 4)])
        load_weight_blocks(0, HH_BLOCKS)
        for t in range(1, COL_TILES):
            load_weight_blocks(t, range(len(BLOCKS)))

        def flip(words):
            flipped, number = new_bank()
            for c in range(CHUNKS):
                cols = slice(c * P, (c + 1) * P)
                nc.tensor.transpose(flipped[:, cols], words[:, cols], ident[:])
            return flipped

        def regroup(copy, grouped, flipped):
            copy(
                out=grouped.bitcast(F32).rearrange("p (g r u) -> p g r u", g=PASSES, u=2),
                in_=flipped[:].rearrange("p (g u r) -> p g r u", g=PASSES, u=2),
            )

        act_codes = {}
        act_scales = {}
        act_grouped = {}
        for src in ("ih", "hh"):
            grouped = acts.tile([P, ROW_TILES * 4 * PASSES * P], BF16, align_bytes=64, name="act_grouped_" + src)
            codes = acts.tile([P, PASSES * BATCH], U32, align_bytes=64, name="act_codes_" + src)
            scales = acts.tile([P, PASSES * BATCH], U8, align_bytes=64, name="act_scales_" + src)
            act_grouped[src] = grouped
            act_codes[src] = codes
            act_scales[src] = scales

        def prepare_rows(src, m, copy):
            flipped = flip(act_rows[src][:, m, :].bitcast(F32))
            grouped = act_grouped[src][:, m * K : (m + 1) * K]
            regroup(copy, grouped, flipped)
            for g in range(PASSES):
                cols = slice(g * BATCH + m * P, g * BATCH + (m + 1) * P)
                nc.vector.quantize_mx(
                    out=act_codes[src][:, cols].bitcast(FP8X4),
                    scales=act_scales[src][:, cols],
                    in_=grouped[:, g * 4 * P : (g + 1) * 4 * P],
                )

        bias = const.tile([P, 2, 16], F32)

        bias_parted = const.tile([P, 2, P], F32)

        def part_biases():
            nc.vector.tensor_copy(out=bias_parted[:], in_=bias_rows[:].rearrange("r (p e) -> r e p", e=2))

        def transpose_biases():
            bias_bank, number = new_bank()
            for e in range(2):
                nc.tensor.transpose(bias_bank[:, e * P : (e + 1) * P], bias_parted[:, e, :], ident[:])
            by_row = bias_bank[:, 0 : 2 * P].rearrange("p (e r) -> p e r", e=2)
            nc.vector.tensor_copy(out=bias[:], in_=by_row[:, :, 0:16])
            z_rows = slice(4 * GATE_Z, 4 * GATE_Z + 4)
            nc.vector.tensor_scalar(out=bias[:, :, z_rows], in0=by_row[:, :, z_rows], scalar1=-1.0, scalar2=None, op0=ALU.mult)

        def bias_of(t, row):
            c, e = divmod(t, 2)
            return bias[:, e, row + c : row + c + 1]

        ALL = slice(0, ROW_TILES)

        w_codes = []
        w_scales = []
        flipped_blocks = {}
        grouped_pairs = {}

        def flip_block(t, pos):
            flipped_blocks[pos] = flip(w_rows[t][:].bitcast(F32)[:, pos * WORDS : (pos + 1) * WORDS])

        def regroup_block(pos, copy=nc.scalar.copy):
            if pos // 2 not in grouped_pairs:
                grouped = stage.tile([P, 2 * K], BF16, align_bytes=64)
                grouped_pairs[pos // 2] = grouped
            half = slice(pos % 2 * K, (pos % 2 + 1) * K)
            regroup(copy, grouped_pairs[pos // 2][:, half], flipped_blocks.pop(pos))

        def new_codes():
            codes = quantised.tile([P, len(BLOCKS) * BLOCK_WORDS], U32, align_bytes=64, tag="w_codes")
            scales = quantised.tile([P, len(BLOCKS) * BLOCK_WORDS], U8, align_bytes=64, tag="w_scales")
            w_codes.append(codes)
            w_scales.append(scales)

        def quantise(t, first, last, grouped):
            cols = slice(first * BLOCK_WORDS, last * BLOCK_WORDS)
            nc.vector.quantize_mx(out=w_codes[t][:, cols].bitcast(FP8X4), scales=w_scales[t][:, cols], in_=grouped)

        def quantise_pair(t, q):
            quantise(t, 2 * q, 2 * q + 2, grouped_pairs.pop(q)[:])

        def multiply(t, gate, sources, total=None, last=True, hold=False, tiles=ALL, opens=False):
            first_pass = total is None
            if first_pass:
                total, number = new_bank()
                if hold:
                    held.add(number)
            passes = [(src, g) for src in sources for g in range(PASSES)]
            for i, (src, g) in enumerate(passes):
                first = BLOCKS.index((src, gate)) * BLOCK_WORDS + g * P
                w_cols = slice(first, first + P)
                a_cols = slice(g * BATCH + tiles.start * P, g * BATCH + tiles.stop * P)
                nc.tensor.matmul_mx(
                    out=total[:, tiles.start * P : tiles.stop * P],
                    lhsT=w_codes[t][:, w_cols].bitcast(FP8X4),
                    lhsT_scale=w_scales[t][:, w_cols],
                    rhs=act_codes[src][:, a_cols].bitcast(FP8X4),
                    rhs_scale=act_scales[src][:, a_cols],
                    start=((first_pass or opens) and i == 0),
                    stop=(last and i == len(passes) - 1),
                )
            return total

        hp_flipped = act_grouped["hh"][:].rearrange(
            "p (m g r u e) -> p g u e m r", m=ROW_TILES, g=PASSES, u=2, e=2
        )
        sums = {}
        gate_tiles = {}
        step = {}

        def gate_tile(name):
            made = gates.tile([P, BATCH], F32, tag=name, name=name)
            gate_tiles[name] = made

        def rows_of(tiles):
            return slice(tiles.start * P, tiles.stop * P)

        def reset_gate(t, tiles=ALL):
            rows = rows_of(tiles)
            nc.scalar.activation(
                out=gate_tiles["reset"][:, rows], in_=sums["r"][:, rows], func=ACT.Sigmoid, bias=bias_of(t, 4 * GATE_R)
            )

        def gated_sum(t, tiles=ALL):
            rows = rows_of(tiles)
            nc.vector.scalar_tensor_tensor(
                out=gate_tiles["gated"][:, rows],
                in0=sums["hn"][:, rows],
                scalar=bias_of(t, 12),
                in1=gate_tiles["reset"][:, rows],
                op0=ALU.add,
                op1=ALU.mult,
            )

        def before_tanh(t, tiles=ALL):
            rows = rows_of(tiles)
            nc.vector.tensor_tensor(
                out=gate_tiles["pre"][:, rows], in0=sums["in"][:, rows], in1=gate_tiles["gated"][:, rows], op=ALU.add
            )

        def new_gate(t, tiles=ALL):
            rows = rows_of(tiles)
            nc.scalar.activation(
                out=gate_tiles["new"][:, rows], in_=gate_tiles["pre"][:, rows], func=ACT.Tanh, bias=bias_of(t, 4 * GATE_N)
            )

        def update_gate(t, tiles=ALL):
            rows = rows_of(tiles)
            nc.scalar.activation(
                out=gate_tiles["keep"][:, rows], in_=sums["z"][:, rows], func=ACT.Sigmoid, bias=bias_of(t, 4 * GATE_Z), scale=-1.0
            )

        def blend_diff(t, tiles=ALL, engine=nc.vector):
            if tiles.start == 0:
                gate_tile("diff")
            rows = rows_of(tiles)
            c, e = divmod(t, 2)
            g, u = divmod(c, 2)
            engine.tensor_tensor(
                out=gate_tiles["diff"][:, rows].rearrange("p (m r) -> p m r", r=P),
                in0=gate_tiles["new"][:, rows].rearrange("p (m r) -> p m r", r=P),
                in1=hp_flipped[:, g, u, e, tiles],
                op=ALU.subtract,
            )

        def blend_step(t, tiles=ALL, engine=nc.vector):
            if t not in step:
                step_t = steps.tile([P, BATCH], F32)
                step[t] = step_t
            rows = rows_of(tiles)
            engine.tensor_tensor(
                out=step[t][:, rows], in0=gate_tiles["keep"][:, rows], in1=gate_tiles["diff"][:, rows], op=ALU.mult
            )

        hp_by_tile = act_rows["hh"]
        out_by_tile = out.rearrange("(p m) j -> p m j", m=ROW_TILES)

        def new_back():
            banks = []
            for half in range(2):
                back, number = new_bank()
                banks.append(back)
            return banks

        def flip_back(banks, t, tiles=ALL):
            for m in range(tiles.start, tiles.stop):
                place = (2 * (m % 2) + t % 2) * P
                nc.tensor.transpose(banks[m // 2][:, place : place + P], step[t][:, m * P : (m + 1) * P], ident[:])

        def add_back(result, banks, c, half):
            tiles = slice(2 * half, 2 * half + 2)
            cols = slice(c * 2 * P, (c + 1) * 2 * P)
            nc.vector.tensor_tensor(
                out=result[:, tiles, :].rearrange("p m (j e) -> p m j e", e=2),
                in0=hp_by_tile[:, tiles, cols].rearrange("p m (j e) -> p m j e", e=2),
                in1=banks[half][:].rearrange("p (m e j) -> p m j e", m=2, e=2),
                op=ALU.add,
            )

        def sum_back(bank, c, m):
            cols = slice(c * 2 * P, (c + 1) * 2 * P)
            parted = act_rows["hh"][:, m, cols].rearrange("p (j e) -> p e j", e=2)
            nc.tensor.matmul(bank[:, 0 : 2 * P], lhsT=ident_bf16[:], rhs=parted, start=True, stop=False)

        def sum_step(bank, t, m):
            nc.tensor.matmul(
                bank[:, t % 2 * P : (t % 2 + 1) * P],
                lhsT=step[t][:, m * P : (m + 1) * P],
                rhs=ident[:],
                is_transpose=True,
                start=False,
                stop=(t % 2 == 1),
            )

        def empty_bank(copy, result, bank, m):
            copy(
                out=result[:, m, :].rearrange("p (j e) -> p j e", e=2),
                in_=bank[:, 0 : 2 * P].rearrange("p (e j) -> p j e", e=2),
            )

        def store(result, c, tiles):
            cols = slice(c * 2 * P, (c + 1) * 2 * P)
            nc.sync.dma_start(out=out_by_tile[:, tiles, cols], in_=result[:, tiles, :])

        for m in range(ROW_TILES):
            prepare_rows("ih", m, nc.scalar.copy)
        new_codes()
        for pos in IH_BLOCKS:
            flip_block(0, pos)
            regroup_block(pos)
            quantise(0, pos, pos + 1, grouped_pairs[pos // 2][:, pos % 2 * K : (pos % 2 + 1) * K])
        keep_warm(2)
        part_biases()
        for m in range(2):
            prepare_rows("hh", m, nc.vector.tensor_copy if m == 1 else nc.scalar.copy)
        sums["r"] = multiply(0, GATE_R, ("ih",), last=False, hold=True)
        sums["in"] = multiply(0, GATE_N, ("ih",), hold=True)
        sums["z"] = multiply(0, GATE_Z, ("ih",), last=False, hold=True)
        for m in range(2, ROW_TILES):
            prepare_rows("hh", m, nc.scalar.copy)
        for pos in HH_BLOCKS:
            flip_block(0, pos)
            regroup_block(pos)
            quantise(0, pos, pos + 1, grouped_pairs[pos // 2][:, pos % 2 * K : (pos % 2 + 1) * K])
        transpose_biases()
        grouped_pairs.clear()

        new_codes()
        for pos in range(2):
            flip_block(1, pos)
            regroup_block(pos)
            if pos % 2 == 1:
                quantise_pair(1, pos // 2)
        multiply(0, GATE_R, ("hh",), total=sums["r"])
        gate_tile("reset")
        gate_tile("gated")
        gate_tile("pre")
        reset_gate(0)
        sums["hn"] = multiply(0, GATE_N, ("hh",), hold=True)
        gated_sum(0)
        before_tanh(0)
        multiply(0, GATE_Z, ("hh",), total=sums["z"])
        gate_tile("keep")
        gate_tile("new")
        for i, pos in enumerate(range(2, len(BLOCKS))):
            flip_block(1, pos)
            regroup_block(pos, nc.vector.tensor_copy if pos in (3, 5) else nc.scalar.copy)
            if i == 0:
                update_gate(0)
            if i == 1:
                new_gate(0)
            if i == 2:
                blend_diff(0)
            if pos % 2 == 1:
                quantise_pair(1, pos // 2)
        held.clear()
        blend_step(0)
        back_banks = []
        back_result = gates.tile([P, ROW_TILES, 2 * P], F32, name="back_result")

        def back_pair(c, half):
            for m in range(2 * half, 2 * half + 2):
                back, number = new_bank()
                back_banks.append(back)
                sum_back(back, c, m)
            for m in range(2 * half, 2 * half + 2):
                sum_step(back_banks[m], 2 * c, m)
                sum_step(back_banks[m], 2 * c + 1, m)

        def empty_back(c, half):
            tiles = slice(2 * half, 2 * half + 2)
            for m in range(2 * half, 2 * half + 2):
                empty_bank(nc.scalar.copy, back_result, back_banks[m], m)
            store(back_result, c, tiles)

        for t in range(1, COL_TILES):
            c, e = divmod(t, 2)
            more = t + 1 < COL_TILES
            done = t - 1
            if more:
                new_codes()
            if e == 1 and c > 0 and more:
                banks = new_back()
                flip_back(banks, t - 3)
                flip_back(banks, t - 2)
                result = gates.tile([P, ROW_TILES, 2 * P], F32)
                add_back(result, banks, c - 1, 0)
                add_back(result, banks, c - 1, 1)
                store(result, c - 1, ALL)
            if not more:
                banks = new_back()
                flip_back(banks, t - 3)
                flip_back(banks, t - 2)
                result = gates.tile([P, ROW_TILES, 2 * P], F32)
                add_back(result, banks, PAIRS - 2, 0)
                add_back(result, banks, PAIRS - 2, 1)
                store(result, PAIRS - 2, ALL)
            if done > 0:
                gate_tile("keep")
                update_gate(done)
            if more:
                flip_block(t + 1, 0)
                regroup_block(0)
            if done > 0:
                gate_tile("new")
                new_gate(done)
            if done > 0:
                blend_diff(done, engine=nc.vector if more else nc.gpsimd)
            if more:
                flip_block(t + 1, 1)
                regroup_block(1)
                quantise_pair(t + 1, 0)
            if done > 0 and more:
                blend_step(done)
            if more:
                flip_block(t + 1, 2)
                regroup_block(2)
                flip_block(t + 1, 3)
                regroup_block(3)
                quantise_pair(t + 1, 1)
                flip_block(t + 1, 4)
                flip_block(t + 1, 5)
            sums["r"] = multiply(t, GATE_R, ("ih", "hh"))
            gate_tile("reset")
            gate_tile("gated")
            gate_tile("pre")
            halves = [ALL] if more else [slice(0, 2), slice(2, 4)]
            for tiles in halves:
                reset_gate(t, tiles)
            if more:
                regroup_block(4)
                regroup_block(5)
            sums["hn"] = multiply(t, GATE_N, ("hh",))
            for tiles in halves:
                gated_sum(t, tiles)
            sums["in"] = multiply(t, GATE_N, ("ih",))
            for tiles in halves:
                before_tanh(t, tiles)
            if more:
                quantise_pair(t + 1, 2)
            if not more:
                blend_step(done, engine=nc.gpsimd)
                gate_tile("new")
                new_gate(t, halves[0])
                new_gate(t, halves[1])
                blend_diff(t, halves[0])
                blend_diff(t, halves[1])
            sums["z"] = multiply(t, GATE_Z, ("ih", "hh"))

        t = COL_TILES - 1
        c = PAIRS - 1
        result = gates.tile([P, ROW_TILES, 2 * P], F32)
        gate_tile("keep")
        for tiles in halves:
            update_gate(t, tiles)
        for m in range(ROW_TILES):
            back, number = new_bank()
            back_banks.append(back)
            sum_back(back, c, m)
        for m in range(ROW_TILES):
            sum_step(back_banks[m], t - 1, m)
        for half, tiles in enumerate(halves):
            blend_step(t, tiles)
            for m in range(tiles.start, tiles.stop):
                sum_step(back_banks[m], t, m)
        for m in range(ROW_TILES):
            empty_bank(nc.scalar.copy if m % 2 == 0 else nc.vector.tensor_copy, result, back_banks[m], m)
            store(result, c, slice(m, m + 1))
